import numpy as np
import ml_dtypes


def mxq(x, axis, fmt="e4m3"):
    dtype, down = {"e4m3": (ml_dtypes.float8_e4m3fn, 7), "e5m2": (ml_dtypes.float8_e5m2, 14)}[fmt]
    v = np.moveaxis(np.asarray(x, np.float32).astype(ml_dtypes.bfloat16).astype(np.float64), axis, -1)
    blocks = v.reshape(v.shape[:-1] + (-1, 32))
    amax = np.abs(blocks).max(-1, keepdims=True)
    byte = np.maximum(np.where(amax > 0, np.frexp(amax)[1] - 1 + 127, 0) - down, 1)
    scale = np.exp2(byte - 127.0)
    codes = (blocks / scale).astype(np.float32).astype(dtype).astype(np.float64)
    return np.moveaxis((codes * scale).reshape(v.shape), -1, axis)


WIDE = False


def mx_kscale(k):
    if not WIDE:
        return np.ones(k)
    levels = np.array([10, -10, 5, -5, 0])
    a = np.random.permutation(np.resize(levels, k // 512 * 4)).reshape(k // 512, 4)
    idx = np.arange(k)
    return np.exp2(a[idx // 512, idx % 128 // 32])


BF16 = ml_dtypes.bfloat16


def bf(x):
    return np.asarray(x, np.float32).astype(BF16)


def f64(x):
    return np.asarray(x).astype(np.float64)


E2M1 = np.array([0.0, 0.5, 1.0, 1.5, 2.0, 3.0, 4.0, 6.0, -0.0, -0.5, -1.0, -1.5, -2.0, -3.0, -4.0, -6.0])


def pack_weight(w, fmt):
    k, n = w.shape
    w = f64(bf(w)).reshape(k // 32, 32, n)
    amax = np.abs(w).max(1)
    if fmt == "e4m3":
        byte = np.frexp(amax)[1] - 1 + 127 - 7
    else:
        mant, ex = np.frexp(amax / 6.0)
        byte = np.where(mant > 0.5, ex, ex - 1) + 127
    byte = np.clip(np.where(amax > 0, byte, 1), 1, 254)
    scaled = (w * np.exp2(127.0 - byte)[:, None, :]).reshape(k, n).astype(np.float32)
    by_word = np.ascontiguousarray(scaled.reshape(k // 512, 128, 4, n).transpose(0, 1, 3, 2))
    if fmt == "e4m3":
        words = by_word.astype(ml_dtypes.float8_e4m3fn).view(np.uint8)
    else:
        c = by_word.astype(ml_dtypes.float4_e2m1fn).view(np.uint8) & 0xF
        words = c[..., 0::2] | (c[..., 1::2] << 4)
    return np.ascontiguousarray(words), np.ascontiguousarray(byte.astype(np.uint8).reshape(k // 512, 16, n))


def unpack_weight(words, scales, fmt):
    g, p, n, _ = words.shape
    if fmt == "e4m3":
        vals = np.ascontiguousarray(words).view(ml_dtypes.float8_e4m3fn).astype(np.float64)
    else:
        nib = np.empty((g, p, n, 4), np.uint8)
        nib[..., 0::2] = words & 0xF
        nib[..., 1::2] = words >> 4
        vals = E2M1[nib]
    vals = vals * np.repeat(np.exp2(scales.astype(np.float64) - 127.0), 8, axis=1)[..., None]
    return vals.transpose(0, 1, 3, 2).reshape(g * 512, n)


B, K, DIM, MEM = 2048, 4, 512, 512
FMT = "e4m3"


def sigmoid(v):
    return 1.0 / (1.0 + np.exp(-v))


def lin(vq, words, scales, b):
    return (vq @ unpack_weight(words, scales, FMT)) + f64(b)


def setup_inputs():
    s, r, t = mx_kscale(DIM), mx_kscale(MEM), mx_kscale(MEM)
    d = {"inputs": bf(np.random.standard_normal((B, DIM)) * s),
         "child_c": bf(np.random.standard_normal((K, B, MEM))),
         "child_h": bf(np.random.standard_normal((K, B, MEM)) * t),
         "child_h_sum": bf(np.random.standard_normal((B, MEM)) * r)}
    for n in ("ix", "fx", "ux", "ox"):
        w = np.random.standard_normal((MEM, DIM)) * 0.7 / np.sqrt(DIM) / s
        d["W_" + n + "_words"], d["W_" + n + "_scales"] = pack_weight(w.T, FMT)
        d["b_" + n] = bf(np.random.standard_normal(MEM) * 0.5)
    for n in ("ih", "fh", "uh", "oh"):
        w = np.random.standard_normal((MEM, MEM)) * 0.7 / np.sqrt(MEM) / (t if n == "fh" else r)
        d["W_" + n + "_words"], d["W_" + n + "_scales"] = pack_weight(w.T, FMT)
        d["b_" + n] = bf(np.random.standard_normal(MEM) * 0.5)
    return d


def reference(inputs, child_c, child_h, child_h_sum,
              W_ix_words, W_ix_scales, b_ix, W_fx_words, W_fx_scales, b_fx,
              W_ux_words, W_ux_scales, b_ux, W_ox_words, W_ox_scales, b_ox,
              W_ih_words, W_ih_scales, b_ih, W_fh_words, W_fh_scales, b_fh,
              W_uh_words, W_uh_scales, b_uh, W_oh_words, W_oh_scales, b_oh):
    xq = mxq(f64(inputs), 1, "e4m3")
    sq = mxq(f64(child_h_sum), 1, "e4m3")
    hq = mxq(f64(child_h), 2, "e4m3")
    i = sigmoid(lin(xq, W_ix_words, W_ix_scales, b_ix) + lin(sq, W_ih_words, W_ih_scales, b_ih))
    o = sigmoid(lin(xq, W_ox_words, W_ox_scales, b_ox) + lin(sq, W_oh_words, W_oh_scales, b_oh))
    u = np.tanh(lin(xq, W_ux_words, W_ux_scales, b_ux) + lin(sq, W_uh_words, W_uh_scales, b_uh))
    fx = lin(xq, W_fx_words, W_fx_scales, b_fx)
    f = sigmoid(lin(hq, W_fh_words, W_fh_scales, b_fh) + fx[None])
    fc = f * f64(child_c)
    c = i * u + fc.sum(axis=0)
    h = o * np.tanh(c)
    return (c, h)

@@ -1,0 +1,297 @@
+from contextlib import ExitStack
+
+import concourse.mybir as mybir
+from concourse.masks import make_identity
+
+F32 = mybir.dt.float32
+BF16 = mybir.dt.bfloat16
+I32 = mybir.dt.int32
+U32 = mybir.dt.uint32
+U8 = mybir.dt.uint8
+FP8X4 = mybir.dt.float8_e4m3fn_x4
+ACT = mybir.ActivationFunctionType
+ALU = mybir.AluOpType
+
+P = 128
+NODES, FEAT, KIDS = 2048, 512, 4
+PACK = 4
+ROWS = NODES // P
+BLOCK = 512
+TILES = BLOCK // P
+BLOCKS = NODES // BLOCK
+FTILES = FEAT // P
+STEPS = BLOCKS * FTILES
+WORDS = FEAT // 2
+
+GATE_I, GATE_F, GATE_U, GATE_O = 0, 1, 2, 3
+GATES = 4
+X_SIDE, H_SIDE = 0, 1
+
+OP_X, OP_KID0, OP_SUM = 0, 1, 1 + KIDS
+OPERANDS = 2 + KIDS
+HALF = BLOCK // 2
+UNITS = 2 * OPERANDS
+UNITS_PER_STEP = UNITS // FTILES
+
+FLOPS = 2 * FEAT * FEAT * (7 * NODES + KIDS * NODES)
+
+
+def tile_treelstm_pa_t_kernel(
+    tc, inputs, child_c, child_h, child_h_sum,
+    W_ix_words, W_ix_scales, b_ix, W_fx_words, W_fx_scales, b_fx,
+    W_ux_words, W_ux_scales, b_ux, W_ox_words, W_ox_scales, b_ox,
+    W_ih_words, W_ih_scales, b_ih, W_fh_words, W_fh_scales, b_fh,
+    W_uh_words, W_uh_scales, b_uh, W_oh_words, W_oh_scales, b_oh,
+    out_0, out_1,
+):
+    nc = tc.nc
+    given_words = [W_ix_words, W_fx_words, W_ux_words, W_ox_words, W_ih_words, W_fh_words, W_uh_words, W_oh_words]
+    given_scales = [W_ix_scales, W_fx_scales, W_ux_scales, W_ox_scales, W_ih_scales, W_fh_scales, W_uh_scales, W_oh_scales]
+    given_bias = [b_ix, b_fx, b_ux, b_ox, b_ih, b_fh, b_uh, b_oh]
+
+    kid_h_rows = child_h.rearrange("k (p r) d -> k p r d", r=ROWS)
+    kid_c_rows = child_c.rearrange("k (p r) d -> k p r d", r=ROWS)
+    operand_rows = (
+        [inputs.rearrange("(p r) d -> p r d", r=ROWS)]
+        + [kid_h_rows[k] for k in range(KIDS)]
+        + [child_h_sum.rearrange("(p r) d -> p r d", r=ROWS)]
+    )
+    c_rows = out_0.rearrange("(p r) d -> p r d", r=ROWS)
+    h_rows = out_1.rearrange("(p r) d -> p r d", r=ROWS)
+
+    with ExitStack() as ctx:
+        const = ctx.enter_context(tc.tile_pool(name="const", bufs=1))
+        loads = ctx.enter_context(tc.tile_pool(name="loads", bufs=2))
+        regroup = ctx.enter_context(tc.tile_pool(name="regroup", bufs=4))
+        quant = ctx.enter_context(tc.tile_pool(name="quant", bufs=2))
+        work = ctx.enter_context(tc.tile_pool(name="work", bufs=2))
+        stores = ctx.enter_context(tc.tile_pool(name="stores", bufs=3))
+        mx_banks = ctx.enter_context(tc.psum_pool(name="mx_banks", bufs=4))
+        tp_banks = ctx.enter_context(tc.psum_pool(name="tp_banks", bufs=4))
+        ctx.enter_context(tc.manual_schedule())
+
+        w_words = const.tile([P, 2 * GATES, FEAT], U32, name="w_words", align_bytes=64)
+        w_scales = const.tile([P, 2 * GATES, FEAT], U8, name="w_scales", align_bytes=64)
+        ident_f32 = const.tile([P, P], F32, name="ident_f32")
+        ident_bf16 = const.tile([P, P], BF16, name="ident_bf16")
+        bias_rows = const.tile([P, P], BF16, name="bias_rows")
+        bias_cols = const.tile([P, 2, GATES * FTILES], F32, name="bias_cols")
+        bias = const.tile([P, GATES, FTILES], F32, name="bias")
+        warm = const.tile([P, 2], F32, name="warm")
+
+        nc.vector.memset(w_scales[:].bitcast(I32), 0)
+        nc.vector.memset(bias_rows[:], 0.0)
+        nc.vector.memset(warm[:], 0.0)
+        nc.scalar.activation(out=warm[:, 1:2], in_=warm[:, 0:1], func=ACT.Sigmoid)
+        make_identity(nc, ident_f32[:])
+        make_identity(nc, ident_bf16[:])
+
+        def load_operands(b):
+            tile = loads.tile([P, OPERANDS, TILES, FEAT], BF16, name="operands")
+            for a in range(OPERANDS):
+                nc.sync.dma_start(out=tile[:, a, :, :], in_=operand_rows[a][:, b * TILES : (b + 1) * TILES, :])
+            return tile
+
+        def load_cells(b):
+            tile = loads.tile([P, KIDS, TILES, FEAT], BF16, name="cells")
+            for k in range(KIDS):
+                nc.sync.dma_start(out=tile[:, k, :, :], in_=kid_c_rows[k][:, b * TILES : (b + 1) * TILES, :])
+            return tile
+
+        def load_weight(slot):
+            nc.sync.dma_start(
+                out=w_words[:, slot, :].bitcast(I32),
+                in_=given_words[slot][0].rearrange("p n t -> p (n t)").bitcast(I32),
+            )
+            scale_rows = given_scales[slot][0].bitcast(I32)
+            for r in range(4):
+                nc.sync.dma_start(out=w_scales[r : P : 32, slot, :].bitcast(I32), in_=scale_rows[r : 16 : 4, :])
+
+        operands = {0: load_operands(0)}
+        load_weight(H_SIDE * GATES + GATE_F)
+        load_weight(X_SIDE * GATES + GATE_F)
+        cells = {0: load_cells(0)}
+        for gate in (GATE_I, GATE_U, GATE_O):
+            load_weight(X_SIDE * GATES + gate)
+            load_weight(H_SIDE * GATES + gate)
+        operands[1] = load_operands(1)
+        for slot in range(2 * GATES):
+            nc.gpsimd.dma_start(
+                out=bias_rows[slot * FTILES : (slot + 1) * FTILES, :],
+                in_=given_bias[slot].rearrange("(m f) -> m f", f=P),
+            )
+
+        q_words = {}
+        q_scales = {}
+
+        def new_quantised(b):
+            q_words[b] = quant.tile([P, OPERANDS, BLOCK], U32, name="q_words", align_bytes=64)
+            q_scales[b] = quant.tile([P, OPERANDS, BLOCK], U8, name="q_scales", align_bytes=64)
+
+        def transpose_unit(b, unit):
+            a, half = divmod(unit, 2)
+            bank = tp_banks.tile([P, 2, 2, P], F32, name="xt", tag="tp")
+            for j in range(2):
+                row_words = operands[b][:, a, 2 * half + j, :].bitcast(F32)
+                for u in range(2):
+                    nc.tensor.transpose(out=bank[:, j, u, :], in_=row_words[:, u:WORDS:2], identity=ident_f32[:])
+            return bank
+
+        def regroup_unit(unit, bank):
+            copy = nc.vector.tensor_copy if unit % UNITS_PER_STEP == UNITS_PER_STEP - 1 else nc.scalar.copy
+            grouped = regroup.tile([P, HALF, PACK], BF16, name="grouped", align_bytes=64)
+            as_words = grouped[:].rearrange("p c t -> p (c t)").bitcast(F32)
+            copy(out=as_words.rearrange("p (j r u) -> p j r u", j=2, u=2), in_=bank[:].rearrange("p j u r -> p j r u"))
+            return grouped
+
+        def quantise_unit(b, unit, grouped):
+            a, half = divmod(unit, 2)
+            cols = slice(half * HALF, (half + 1) * HALF)
+            nc.vector.quantize_mx(
+                out=q_words[b][:, a, cols].bitcast(FP8X4),
+                scales=q_scales[b][:, a, cols],
+                in_=grouped[:].rearrange("p c t -> p (c t)"),
+            )
+
+        live = {}
+
+        def mx_group(t, gate, h_operand):
+            b, m = divmod(t, FTILES)
+            feats = slice(m * P, (m + 1) * P)
+            z = mx_banks.tile([P, BLOCK], F32, name="z")
+            for side, a in ((H_SIDE, h_operand), (X_SIDE, OP_X)):
+                slot = side * GATES + gate
+                nc.tensor.matmul_mx(
+                    out=z[:],
+                    lhsT=w_words[:, slot, feats].bitcast(FP8X4),
+                    lhsT_scale=w_scales[:, slot, feats],
+                    rhs=q_words[b][:, a, :].bitcast(FP8X4),
+                    rhs_scale=q_scales[b][:, a, :],
+                    start=(side == H_SIDE),
+                    stop=(side == X_SIDE),
+                )
+            return z
+
+        def forget_gates(t):
+            m = t % FTILES
+            forget = work.tile([P, KIDS, BLOCK], F32, name="forget")
+            banks = [mx_group(t, GATE_F, OP_KID0 + k) for k in range(KIDS)]
+            for k in range(KIDS):
+                nc.scalar.activation(out=forget[:, k, :], in_=banks[k][:], func=ACT.Sigmoid, bias=bias[:, GATE_F, m : m + 1])
+            live["forget", t] = forget
+
+        def transpose_cells(t):
+            b, m = divmod(t, FTILES)
+            for pair in range(KIDS // 2):
+                bank = tp_banks.tile([P, 2, TILES, P], BF16, name="ct", tag="tp")
+                for k in range(2):
+                    for j in range(TILES):
+                        nc.tensor.transpose(
+                            out=bank[:, k, j, :],
+                            in_=cells[b][:, 2 * pair + k, j, m * P : (m + 1) * P],
+                            identity=ident_bf16[:],
+                        )
+                live["ct", t, pair] = bank
+
+        def products(t):
+            prod = work.tile([P, KIDS, BLOCK], F32, name="prod")
+            for pair in range(KIDS // 2):
+                kids = slice(2 * pair, 2 * pair + 2)
+                nc.vector.tensor_tensor(
+                    out=prod[:, kids, :],
+                    in0=live["forget", t][:, kids, :],
+                    in1=live["ct", t, pair][:].rearrange("p k j r -> p k (j r)"),
+                    op=ALU.mult,
+                )
+            live["prod", t] = prod
+
+        def child_sum(t):
+            prod = live["prod", t]
+            pair_sum = work.tile([P, 2, BLOCK], F32, name="pair_sum")
+            kid_sum = work.tile([P, BLOCK], F32, name="kid_sum")
+            nc.gpsimd.tensor_tensor(out=pair_sum[:], in0=prod[:, 0:2, :], in1=prod[:, 2:4, :], op=ALU.add)
+            nc.gpsimd.tensor_tensor(out=kid_sum[:], in0=pair_sum[:, 0, :], in1=pair_sum[:, 1, :], op=ALU.add)
+            live["kid_sum", t] = kid_sum
+
+        def other_gates_and_cell(t):
+            m = t % FTILES
+            gate_i = work.tile([P, BLOCK], F32, name="gate_i")
+            gate_u = work.tile([P, BLOCK], F32, name="gate_u")
+            gate_o = work.tile([P, BLOCK], F32, name="gate_o")
+            plan = ((GATE_I, gate_i, ACT.Sigmoid), (GATE_U, gate_u, ACT.Tanh), (GATE_O, gate_o, ACT.Sigmoid))
+            banks = [mx_group(t, gate, OP_SUM) for gate, out_tile, func in plan]
+            for bank, (gate, out_tile, func) in zip(banks, plan):
+                nc.scalar.activation(out=out_tile[:], in_=bank[:], func=func, bias=bias[:, gate, m : m + 1])
+            iu = work.tile([P, BLOCK], F32, name="iu")
+            cell = work.tile([P, BLOCK], F32, name="cell")
+            nc.vector.tensor_tensor(out=iu[:], in0=gate_i[:], in1=gate_u[:], op=ALU.mult)
+            nc.gpsimd.tensor_tensor(out=cell[:], in0=live["kid_sum", t][:], in1=iu[:], op=ALU.add)
+            live["gate_o", t] = gate_o
+            live["cell", t] = cell
+
+        def hidden(t):
+            tanh_c = work.tile([P, BLOCK], F32, name="tanh_c")
+            hid = work.tile([P, BLOCK], F32, name="hid")
+            nc.scalar.activation(out=tanh_c[:], in_=live["cell", t][:], func=ACT.Tanh)
+            nc.vector.tensor_tensor(out=hid[:], in0=live["gate_o", t][:], in1=tanh_c[:], op=ALU.mult)
+            live["hid", t] = hid
+
+        def write_back(t):
+            b, m = divmod(t, FTILES)
+            banks = {}
+            for name in ("cell", "hid"):
+                banks[name] = tp_banks.tile([P, TILES, P], F32, name="back", tag="tp")
+                for j in range(TILES):
+                    nc.tensor.transpose(
+                        out=banks[name][:, j, :], in_=live[name, t][:, j * P : (j + 1) * P], identity=ident_f32[:]
+                    )
+            for name, copy, dram in (("cell", nc.scalar.copy, c_rows), ("hid", nc.vector.tensor_copy, h_rows)):
+                node_major = stores.tile([P, TILES, P], F32, name="out_" + name)
+                copy(out=node_major[:], in_=banks[name][:])
+                nc.sync.dma_start(out=dram[:, b * TILES : (b + 1) * TILES, m * P : (m + 1) * P], in_=node_major[:])
+
+        new_quantised(0)
+        waiting = None
+        for unit in range(UNITS):
+            bank = transpose_unit(0, unit)
+            grouped = regroup_unit(unit, bank)
+            if waiting is not None:
+                quantise_unit(0, unit - 1, waiting)
+            waiting = grouped
+        quantise_unit(0, UNITS - 1, waiting)
+
+        bias_bank = tp_banks.tile([P, P], BF16, name="bias_bank", tag="tp")
+        nc.tensor.transpose(out=bias_bank[:], in_=bias_rows[:], identity=ident_bf16[:])
+        nc.vector.tensor_copy(out=bias_cols[:].rearrange("p s c -> p (s c)"), in_=bias_bank[:, 0 : 2 * GATES * FTILES])
+        nc.vector.tensor_tensor(
+            out=bias[:].rearrange("p g m -> p (g m)"), in0=bias_cols[:, X_SIDE, :], in1=bias_cols[:, H_SIDE, :], op=ALU.add
+        )
+
+        for t in range(STEPS + 1):
+            b, m = divmod(t, FTILES)
+            if t < STEPS:
+                if m == 0 and b + 2 < BLOCKS:
+                    operands[b + 2] = load_operands(b + 2)
+                if m == 0 and b + 1 < BLOCKS:
+                    cells[b + 1] = load_cells(b + 1)
+                forget_gates(t)
+                if t == 0:
+                    transpose_cells(0)
+                products(t)
+            if t >= 1:
+                hidden(t - 1)
+            if t < STEPS:
+                if b + 1 < BLOCKS:
+                    if m == 0:
+                        new_quantised(b + 1)
+                    units = range(m * UNITS_PER_STEP, (m + 1) * UNITS_PER_STEP)
+                    banks = [transpose_unit(b + 1, unit) for unit in units]
+                    grouped_units = [regroup_unit(unit, bank) for unit, bank in zip(units, banks)]
+                    for unit, grouped in zip(units, grouped_units):
+                        quantise_unit(b + 1, unit, grouped)
+                child_sum(t)
+                other_gates_and_cell(t)
+            if t >= 1:
+                write_back(t - 1)
+            if t + 1 < STEPS:
+                transpose_cells(t + 1)

@@ -32,6 +32,7 @@ OPERANDS = 2 + KIDS
 HALF = BLOCK // 2
 UNITS = 2 * OPERANDS
 UNITS_PER_STEP = UNITS // FTILES
+AHEAD = 2 * OP_SUM
 
 FLOPS = 2 * FEAT * FEAT * (7 * NODES + KIDS * NODES)
 
@@ -63,11 +64,12 @@ def tile_treelstm_pa_t_kernel(
         const = ctx.enter_context(tc.tile_pool(name="const", bufs=1))
         loads = ctx.enter_context(tc.tile_pool(name="loads", bufs=2))
         regroup = ctx.enter_context(tc.tile_pool(name="regroup", bufs=4))
-        quant = ctx.enter_context(tc.tile_pool(name="quant", bufs=2))
+        quant = ctx.enter_context(tc.tile_pool(name="quant", bufs=3))
         work = ctx.enter_context(tc.tile_pool(name="work", bufs=2))
-        stores = ctx.enter_context(tc.tile_pool(name="stores", bufs=3))
-        mx_banks = ctx.enter_context(tc.psum_pool(name="mx_banks", bufs=4))
-        tp_banks = ctx.enter_context(tc.psum_pool(name="tp_banks", bufs=4))
+        stores = ctx.enter_context(tc.tile_pool(name="stores", bufs=4))
+        mx_banks = ctx.enter_context(tc.psum_pool(name="mx_banks", bufs=3))
+        ct_banks = ctx.enter_context(tc.psum_pool(name="ct_banks", bufs=2))
+        tp_banks = ctx.enter_context(tc.psum_pool(name="tp_banks", bufs=3))
         ctx.enter_context(tc.manual_schedule())
 
         w_words = const.tile([P, 2 * GATES, FEAT], U32, name="w_words", align_bytes=64)
@@ -86,17 +88,20 @@ def tile_treelstm_pa_t_kernel(
         make_identity(nc, ident_f32[:])
         make_identity(nc, ident_bf16[:])
 
-        def load_operands(b):
-            tile = loads.tile([P, OPERANDS, TILES, FEAT], BF16, name="operands")
-            for a in range(OPERANDS):
-                nc.sync.dma_start(out=tile[:, a, :, :], in_=operand_rows[a][:, b * TILES : (b + 1) * TILES, :])
-            return tile
+        operands = {}
+        cells = {}
 
-        def load_cells(b):
-            tile = loads.tile([P, KIDS, TILES, FEAT], BF16, name="cells")
-            for k in range(KIDS):
-                nc.sync.dma_start(out=tile[:, k, :, :], in_=kid_c_rows[k][:, b * TILES : (b + 1) * TILES, :])
-            return tile
+        def new_loads(b):
+            operands[b] = loads.tile([P, OPERANDS, TILES, FEAT], BF16, name="operands")
+
+        def load_operand(b, a):
+            nc.sync.dma_start(out=operands[b][:, a, :, :], in_=operand_rows[a][:, b * TILES : (b + 1) * TILES, :])
+
+        def new_cells(b):
+            cells[b] = loads.tile([P, KIDS, TILES, FEAT], BF16, name="cells")
+
+        def load_cell(b, k):
+            nc.sync.dma_start(out=cells[b][:, k, :, :], in_=kid_c_rows[k][:, b * TILES : (b + 1) * TILES, :])
 
         def load_weight(slot):
             nc.sync.dma_start(
@@ -104,17 +109,29 @@ def tile_treelstm_pa_t_kernel(
                 in_=given_words[slot][0].rearrange("p n t -> p (n t)").bitcast(I32),
             )
             scale_rows = given_scales[slot][0].bitcast(I32)
-            for r in range(4):
-                nc.sync.dma_start(out=w_scales[r : P : 32, slot, :].bitcast(I32), in_=scale_rows[r : 16 : 4, :])
+            for quadrant in range(4):
+                nc.sync.dma_start(
+                    out=w_scales[32 * quadrant : 32 * quadrant + 4, slot, :].bitcast(I32),
+                    in_=scale_rows[4 * quadrant : 4 * quadrant + 4, :],
+                )
 
-        operands = {0: load_operands(0)}
+        new_loads(0)
+        new_cells(0)
+        new_loads(1)
+        for a in range(OP_SUM):
+            load_operand(0, a)
         load_weight(H_SIDE * GATES + GATE_F)
         load_weight(X_SIDE * GATES + GATE_F)
-        cells = {0: load_cells(0)}
-        for gate in (GATE_I, GATE_U, GATE_O):
-            load_weight(X_SIDE * GATES + gate)
+        load_operand(0, OP_SUM)
+        for k in range(KIDS):
+            load_cell(0, k)
+        load_operand(1, OP_X)
+        for n, gate in enumerate((GATE_I, GATE_U, GATE_O)):
             load_weight(H_SIDE * GATES + gate)
-        operands[1] = load_operands(1)
+            load_weight(X_SIDE * GATES + gate)
+            load_operand(1, OP_KID0 + n)
+        load_operand(1, OP_KID0 + 3)
+        load_operand(1, OP_SUM)
         for slot in range(2 * GATES):
             nc.gpsimd.dma_start(
                 out=bias_rows[slot * FTILES : (slot + 1) * FTILES, :],
@@ -128,7 +145,8 @@ def tile_treelstm_pa_t_kernel(
             q_words[b] = quant.tile([P, OPERANDS, BLOCK], U32, name="q_words", align_bytes=64)
             q_scales[b] = quant.tile([P, OPERANDS, BLOCK], U8, name="q_scales", align_bytes=64)
 
-        def transpose_unit(b, unit):
+        def transpose_unit(count):
+            b, unit = divmod(count, UNITS)
             a, half = divmod(unit, 2)
             bank = tp_banks.tile([P, 2, 2, P], F32, name="xt", tag="tp")
             for j in range(2):
@@ -137,15 +155,17 @@ def tile_treelstm_pa_t_kernel(
                     nc.tensor.transpose(out=bank[:, j, u, :], in_=row_words[:, u:WORDS:2], identity=ident_f32[:])
             return bank
 
-        def regroup_unit(unit, bank):
-            copy = nc.vector.tensor_copy if unit % UNITS_PER_STEP == UNITS_PER_STEP - 1 else nc.scalar.copy
+        def regroup_unit(copy, bank):
             grouped = regroup.tile([P, HALF, PACK], BF16, name="grouped", align_bytes=64)
             as_words = grouped[:].rearrange("p c t -> p (c t)").bitcast(F32)
             copy(out=as_words.rearrange("p (j r u) -> p j r u", j=2, u=2), in_=bank[:].rearrange("p j u r -> p j r u"))
             return grouped
 
-        def quantise_unit(b, unit, grouped):
+        def quantise_unit(count, grouped):
+            b, unit = divmod(count, UNITS)
             a, half = divmod(unit, 2)
+            if unit == 0:
+                new_quantised(b)
             cols = slice(half * HALF, (half + 1) * HALF)
             nc.vector.quantize_mx(
                 out=q_words[b][:, a, cols].bitcast(FP8X4),
@@ -172,93 +192,58 @@ def tile_treelstm_pa_t_kernel(
                 )
             return z
 
-        def forget_gates(t):
+        def squash(t, gate, func, z, out):
             m = t % FTILES
-            forget = work.tile([P, KIDS, BLOCK], F32, name="forget")
-            banks = [mx_group(t, GATE_F, OP_KID0 + k) for k in range(KIDS)]
-            for k in range(KIDS):
-                nc.scalar.activation(out=forget[:, k, :], in_=banks[k][:], func=ACT.Sigmoid, bias=bias[:, GATE_F, m : m + 1])
-            live["forget", t] = forget
+            nc.scalar.activation(out=out, in_=z[:], func=func, bias=bias[:, gate, m : m + 1])
 
-        def transpose_cells(t):
+        def transpose_cells(t, pair):
             b, m = divmod(t, FTILES)
-            for pair in range(KIDS // 2):
-                bank = tp_banks.tile([P, 2, TILES, P], BF16, name="ct", tag="tp")
-                for k in range(2):
-                    for j in range(TILES):
-                        nc.tensor.transpose(
-                            out=bank[:, k, j, :],
-                            in_=cells[b][:, 2 * pair + k, j, m * P : (m + 1) * P],
-                            identity=ident_bf16[:],
-                        )
-                live["ct", t, pair] = bank
-
-        def products(t):
-            prod = work.tile([P, KIDS, BLOCK], F32, name="prod")
-            for pair in range(KIDS // 2):
-                kids = slice(2 * pair, 2 * pair + 2)
-                nc.vector.tensor_tensor(
-                    out=prod[:, kids, :],
-                    in0=live["forget", t][:, kids, :],
-                    in1=live["ct", t, pair][:].rearrange("p k j r -> p k (j r)"),
-                    op=ALU.mult,
-                )
-            live["prod", t] = prod
-
-        def child_sum(t):
-            prod = live["prod", t]
-            pair_sum = work.tile([P, 2, BLOCK], F32, name="pair_sum")
-            kid_sum = work.tile([P, BLOCK], F32, name="kid_sum")
-            nc.gpsimd.tensor_tensor(out=pair_sum[:], in0=prod[:, 0:2, :], in1=prod[:, 2:4, :], op=ALU.add)
-            nc.gpsimd.tensor_tensor(out=kid_sum[:], in0=pair_sum[:, 0, :], in1=pair_sum[:, 1, :], op=ALU.add)
-            live["kid_sum", t] = kid_sum
-
-        def other_gates_and_cell(t):
-            m = t % FTILES
-            gate_i = work.tile([P, BLOCK], F32, name="gate_i")
-            gate_u = work.tile([P, BLOCK], F32, name="gate_u")
-            gate_o = work.tile([P, BLOCK], F32, name="gate_o")
-            plan = ((GATE_I, gate_i, ACT.Sigmoid), (GATE_U, gate_u, ACT.Tanh), (GATE_O, gate_o, ACT.Sigmoid))
-            banks = [mx_group(t, gate, OP_SUM) for gate, out_tile, func in plan]
-            for bank, (gate, out_tile, func) in zip(banks, plan):
-                nc.scalar.activation(out=out_tile[:], in_=bank[:], func=func, bias=bias[:, gate, m : m + 1])
-            iu = work.tile([P, BLOCK], F32, name="iu")
-            cell = work.tile([P, BLOCK], F32, name="cell")
-            nc.vector.tensor_tensor(out=iu[:], in0=gate_i[:], in1=gate_u[:], op=ALU.mult)
-            nc.gpsimd.tensor_tensor(out=cell[:], in0=live["kid_sum", t][:], in1=iu[:], op=ALU.add)
-            live["gate_o", t] = gate_o
-            live["cell", t] = cell
-
-        def hidden(t):
-            tanh_c = work.tile([P, BLOCK], F32, name="tanh_c")
-            hid = work.tile([P, BLOCK], F32, name="hid")
-            nc.scalar.activation(out=tanh_c[:], in_=live["cell", t][:], func=ACT.Tanh)
-            nc.vector.tensor_tensor(out=hid[:], in0=live["gate_o", t][:], in1=tanh_c[:], op=ALU.mult)
-            live["hid", t] = hid
-
-        def write_back(t):
-            b, m = divmod(t, FTILES)
-            banks = {}
-            for name in ("cell", "hid"):
-                banks[name] = tp_banks.tile([P, TILES, P], F32, name="back", tag="tp")
+            bank = ct_banks.tile([P, 2, TILES, P], BF16, name="ct")
+            for k in range(2):
                 for j in range(TILES):
                     nc.tensor.transpose(
-                        out=banks[name][:, j, :], in_=live[name, t][:, j * P : (j + 1) * P], identity=ident_f32[:]
+                        out=bank[:, k, j, :],
+                        in_=cells[b][:, 2 * pair + k, j, m * P : (m + 1) * P],
+                        identity=ident_bf16[:],
                     )
-            for name, copy, dram in (("cell", nc.scalar.copy, c_rows), ("hid", nc.vector.tensor_copy, h_rows)):
-                node_major = stores.tile([P, TILES, P], F32, name="out_" + name)
-                copy(out=node_major[:], in_=banks[name][:])
-                nc.sync.dma_start(out=dram[:, b * TILES : (b + 1) * TILES, m * P : (m + 1) * P], in_=node_major[:])
+            live["ct", t, pair] = bank
 
-        new_quantised(0)
+        def products(t, pair):
+            kids = slice(2 * pair, 2 * pair + 2)
+            nc.vector.tensor_tensor(
+                out=live["forget", t][:, kids, :],
+                in0=live["forget", t][:, kids, :],
+                in1=live["ct", t, pair][:].rearrange("p k j r -> p k (j r)"),
+                op=ALU.mult,
+            )
+
+        def finish_cell(t):
+            iu = work.tile([P, BLOCK], F32, name="iu")
+            cell = work.tile([P, BLOCK], F32, name="cell")
+            nc.vector.tensor_tensor(out=iu[:], in0=live["gate_i", t][:], in1=live["gate_u", t][:], op=ALU.mult)
+            nc.vector.tensor_tensor(out=cell[:], in0=live["kid_sum", t][:], in1=iu[:], op=ALU.add)
+            live["cell", t] = cell
+
+        def transpose_back(t, name):
+            bank = tp_banks.tile([P, TILES, P], F32, name="back", tag="tp")
+            for j in range(TILES):
+                nc.tensor.transpose(out=bank[:, j, :], in_=live[name, t][:, j * P : (j + 1) * P], identity=ident_f32[:])
+            return bank
+
+        def store(t, copy, bank, dram):
+            b, m = divmod(t, FTILES)
+            node_major = stores.tile([P, TILES, P], F32, name="node_major")
+            copy(out=node_major[:], in_=bank[:])
+            nc.sync.dma_start(out=dram[:, b * TILES : (b + 1) * TILES, m * P : (m + 1) * P], in_=node_major[:])
+
         waiting = None
-        for unit in range(UNITS):
-            bank = transpose_unit(0, unit)
-            grouped = regroup_unit(unit, bank)
+        for count in range(AHEAD):
+            bank = transpose_unit(count)
+            grouped = regroup_unit(nc.scalar.copy if count % 2 == 0 else nc.vector.tensor_copy, bank)
             if waiting is not None:
-                quantise_unit(0, unit - 1, waiting)
+                quantise_unit(count - 1, waiting)
             waiting = grouped
-        quantise_unit(0, UNITS - 1, waiting)
+        quantise_unit(AHEAD - 1, waiting)
 
         bias_bank = tp_banks.tile([P, P], BF16, name="bias_bank", tag="tp")
         nc.tensor.transpose(out=bias_bank[:], in_=bias_rows[:], identity=ident_bf16[:])
@@ -267,31 +252,85 @@ def tile_treelstm_pa_t_kernel(
             out=bias[:].rearrange("p g m -> p (g m)"), in0=bias_cols[:, X_SIDE, :], in1=bias_cols[:, H_SIDE, :], op=ALU.add
         )
 
-        for t in range(STEPS + 1):
+        for t in range(STEPS + 3):
             b, m = divmod(t, FTILES)
-            if t < STEPS:
-                if m == 0 and b + 2 < BLOCKS:
-                    operands[b + 2] = load_operands(b + 2)
-                if m == 0 and b + 1 < BLOCKS:
-                    cells[b + 1] = load_cells(b + 1)
-                forget_gates(t)
-                if t == 0:
-                    transpose_cells(0)
-                products(t)
-            if t >= 1:
-                hidden(t - 1)
-            if t < STEPS:
-                if b + 1 < BLOCKS:
-                    if m == 0:
-                        new_quantised(b + 1)
-                    units = range(m * UNITS_PER_STEP, (m + 1) * UNITS_PER_STEP)
-                    banks = [transpose_unit(b + 1, unit) for unit in units]
-                    grouped_units = [regroup_unit(unit, bank) for unit, bank in zip(units, banks)]
-                    for unit, grouped in zip(units, grouped_units):
-                        quantise_unit(b + 1, unit, grouped)
-                child_sum(t)
-                other_gates_and_cell(t)
-            if t >= 1:
-                write_back(t - 1)
+            has_f = t < STEPS
+            has_g = 0 <= t - 1 < STEPS
+            has_c = 0 <= t - 2 < STEPS
+            has_s = 0 <= t - 3 < STEPS
+            counts = [c for c in range(AHEAD + t * UNITS_PER_STEP, AHEAD + (t + 1) * UNITS_PER_STEP) if c < BLOCKS * UNITS]
+            if has_f and m == 1 and b + 1 < BLOCKS:
+                new_cells(b + 1)
+                for k in range(KIDS):
+                    load_cell(b + 1, k)
+            if has_f and m == 1 and b + 2 < BLOCKS:
+                new_loads(b + 2)
+                for a in range(OPERANDS):
+                    load_operand(b + 2, a)
+
+            if has_f:
+                live["forget", t] = work.tile([P, KIDS, BLOCK], F32, name="forget")
+                z_forget = [mx_group(t, GATE_F, OP_KID0 + k) for k in range(3)]
+            if has_s:
+                store(t - 3, nc.scalar.copy, live["back_c", t - 3], c_rows)
+                store(t - 3, nc.vector.tensor_copy, live["back_h", t - 3], h_rows)
+            if has_c:
+                finish_cell(t - 2)
+            if has_g:
+                live["kid_sum", t - 1] = work.tile([P, BLOCK], F32, name="kid_sum")
+                pair_sum = live["pair_sum", t - 1]
+                nc.vector.tensor_tensor(out=live["kid_sum", t - 1][:], in0=pair_sum[:, 0, :], in1=pair_sum[:, 1, :], op=ALU.add)
+            if has_f:
+                for k in range(3):
+                    squash(t, GATE_F, ACT.Sigmoid, z_forget[k], live["forget", t][:, k, :])
+            xt = [transpose_unit(count) for count in counts[0:2]]
+            grouped = [regroup_unit(nc.scalar.copy, bank) for bank in xt]
+            if t == 0:
+                transpose_cells(0, 0)
+                transpose_cells(0, 1)
+            if has_f:
+                products(t, 0)
+            for count, tile in zip(counts[0:2], grouped):
+                quantise_unit(count, tile)
+            if has_c:
+                tanh_c = work.tile([P, BLOCK], F32, name="tanh_c")
+                nc.scalar.activation(out=tanh_c[:], in_=live["cell", t - 2][:], func=ACT.Tanh)
+
+            if has_f:
+                z_last = mx_group(t, GATE_F, OP_KID0 + 3)
+            if has_g:
+                live["gate_i", t - 1] = work.tile([P, BLOCK], F32, name="gate_i")
+                z_i = mx_group(t - 1, GATE_I, OP_SUM)
+            xt = [transpose_unit(count) for count in counts[2:3]]
             if t + 1 < STEPS:
-                transpose_cells(t + 1)
+                transpose_cells(t + 1, 0)
+            if has_f:
+                squash(t, GATE_F, ACT.Sigmoid, z_last, live["forget", t][:, 3, :])
+            if has_g:
+                squash(t - 1, GATE_I, ACT.Sigmoid, z_i, live["gate_i", t - 1][:])
+            grouped = [regroup_unit(nc.scalar.copy, bank) for bank in xt]
+            if has_c:
+                live["hid", t - 2] = work.tile([P, BLOCK], F32, name="hid")
+                nc.vector.tensor_tensor(out=live["hid", t - 2][:], in0=live["gate_o", t - 2][:], in1=tanh_c[:], op=ALU.mult)
+            if has_f:
+                products(t, 1)
+                live["pair_sum", t] = work.tile([P, 2, BLOCK], F32, name="pair_sum")
+                nc.gpsimd.tensor_tensor(
+                    out=live["pair_sum", t][:], in0=live["forget", t][:, 0:2, :], in1=live["forget", t][:, 2:4, :], op=ALU.add
+                )
+            for count, tile in zip(counts[2:3], grouped):
+                quantise_unit(count, tile)
+
+            if has_g:
+                live["gate_u", t - 1] = work.tile([P, BLOCK], F32, name="gate_u")
+                live["gate_o", t - 1] = work.tile([P, BLOCK], F32, name="gate_o")
+                z_u = mx_group(t - 1, GATE_U, OP_SUM)
+                z_o = mx_group(t - 1, GATE_O, OP_SUM)
+            if t + 1 < STEPS:
+                transpose_cells(t + 1, 1)
+            if has_c:
+                live["back_c", t - 2] = transpose_back(t - 2, "cell")
+                live["back_h", t - 2] = transpose_back(t - 2, "hid")
+            if has_g:
+                squash(t - 1, GATE_U, ACT.Tanh, z_u, live["gate_u", t - 1][:])
+                squash(t - 1, GATE_O, ACT.Sigmoid, z_o, live["gate_o", t - 1][:])

@@ -230,10 +230,10 @@ def tile_treelstm_pa_t_kernel(
                 nc.tensor.transpose(out=bank[:, j, :], in_=live[name, t][:, j * P : (j + 1) * P], identity=ident_f32[:])
             return bank
 
-        def store(t, copy, bank, dram):
+        def store(t, bank, dram):
             b, m = divmod(t, FTILES)
             node_major = stores.tile([P, TILES, P], F32, name="node_major")
-            copy(out=node_major[:], in_=bank[:])
+            nc.scalar.copy(out=node_major[:], in_=bank[:])
             nc.sync.dma_start(out=dram[:, b * TILES : (b + 1) * TILES, m * P : (m + 1) * P], in_=node_major[:])
 
         waiting = None
@@ -272,8 +272,8 @@ def tile_treelstm_pa_t_kernel(
                 live["forget", t] = work.tile([P, KIDS, BLOCK], F32, name="forget")
                 z_forget = [mx_group(t, GATE_F, OP_KID0 + k) for k in range(3)]
             if has_s:
-                store(t - 3, nc.scalar.copy, live["back_c", t - 3], c_rows)
-                store(t - 3, nc.vector.tensor_copy, live["back_h", t - 3], h_rows)
+                store(t - 3, live["back_c", t - 3], c_rows)
+                store(t - 3, live["back_h", t - 3], h_rows)
             if has_c:
                 finish_cell(t - 2)
             if has_g:
@@ -283,14 +283,14 @@ def tile_treelstm_pa_t_kernel(
             if has_f:
                 for k in range(3):
                     squash(t, GATE_F, ACT.Sigmoid, z_forget[k], live["forget", t][:, k, :])
-            xt = [transpose_unit(count) for count in counts[0:2]]
+            xt = [transpose_unit(count) for count in counts[0:1]]
             grouped = [regroup_unit(nc.scalar.copy, bank) for bank in xt]
             if t == 0:
                 transpose_cells(0, 0)
-                transpose_cells(0, 1)
             if has_f:
+                transpose_cells(t, 1)
                 products(t, 0)
-            for count, tile in zip(counts[0:2], grouped):
+            for count, tile in zip(counts[0:1], grouped):
                 quantise_unit(count, tile)
             if has_c:
                 tanh_c = work.tile([P, BLOCK], F32, name="tanh_c")
@@ -301,9 +301,7 @@ def tile_treelstm_pa_t_kernel(
             if has_g:
                 live["gate_i", t - 1] = work.tile([P, BLOCK], F32, name="gate_i")
                 z_i = mx_group(t - 1, GATE_I, OP_SUM)
-            xt = [transpose_unit(count) for count in counts[2:3]]
-            if t + 1 < STEPS:
-                transpose_cells(t + 1, 0)
+            xt = [transpose_unit(count) for count in counts[1:3]]
             if has_f:
                 squash(t, GATE_F, ACT.Sigmoid, z_last, live["forget", t][:, 3, :])
             if has_g:
@@ -315,10 +313,10 @@ def tile_treelstm_pa_t_kernel(
             if has_f:
                 products(t, 1)
                 live["pair_sum", t] = work.tile([P, 2, BLOCK], F32, name="pair_sum")
-                nc.gpsimd.tensor_tensor(
+                nc.vector.tensor_tensor(
                     out=live["pair_sum", t][:], in0=live["forget", t][:, 0:2, :], in1=live["forget", t][:, 2:4, :], op=ALU.add
                 )
-            for count, tile in zip(counts[2:3], grouped):
+            for count, tile in zip(counts[1:3], grouped):
                 quantise_unit(count, tile)
 
             if has_g:
@@ -327,7 +325,7 @@ def tile_treelstm_pa_t_kernel(
                 z_u = mx_group(t - 1, GATE_U, OP_SUM)
                 z_o = mx_group(t - 1, GATE_O, OP_SUM)
             if t + 1 < STEPS:
-                transpose_cells(t + 1, 1)
+                transpose_cells(t + 1, 0)
             if has_c:
                 live["back_c", t - 2] = transpose_back(t - 2, "cell")
                 live["back_h", t - 2] = transpose_back(t - 2, "hid")

@@ -76,7 +76,7 @@ def tile_treelstm_pa_t_kernel(
         w_scales = const.tile([P, 2 * GATES, FEAT], U8, name="w_scales", align_bytes=64)
         ident_f32 = const.tile([P, P], F32, name="ident_f32")
         ident_bf16 = const.tile([P, P], BF16, name="ident_bf16")
-        bias_rows = const.tile([P, P], BF16, name="bias_rows")
+        bias_rows = const.tile([P, 2, P], BF16, name="bias_rows")
         bias_cols = const.tile([P, 2, GATES * FTILES], F32, name="bias_cols")
         bias = const.tile([P, GATES, FTILES], F32, name="bias")
         warm = const.tile([P, 2], F32, name="warm")
@@ -86,7 +86,7 @@ def tile_treelstm_pa_t_kernel(
         nc.vector.memset(warm[:], 0.0)
         nc.scalar.activation(out=warm[:, 1:2], in_=warm[:, 0:1], func=ACT.Sigmoid)
         make_identity(nc, ident_f32[:])
-        make_identity(nc, ident_bf16[:])
+        nc.scalar.copy(out=ident_bf16[:], in_=ident_f32[:])
 
         operands = {}
         cells = {}
@@ -108,35 +108,39 @@ def tile_treelstm_pa_t_kernel(
                 out=w_words[:, slot, :].bitcast(I32),
                 in_=given_words[slot][0].rearrange("p n t -> p (n t)").bitcast(I32),
             )
-            scale_rows = given_scales[slot][0].bitcast(I32)
-            for quadrant in range(4):
-                nc.sync.dma_start(
-                    out=w_scales[32 * quadrant : 32 * quadrant + 4, slot, :].bitcast(I32),
-                    in_=scale_rows[4 * quadrant : 4 * quadrant + 4, :],
-                )
+
+        def load_scales(slot, quadrant):
+            nc.sync.dma_start(
+                out=w_scales[32 * quadrant : 32 * quadrant + 4, slot, :].bitcast(I32),
+                in_=given_scales[slot][0].bitcast(I32)[4 * quadrant : 4 * quadrant + 4, :],
+            )
+
+        def load_bias(queue, group, row, slot):
+            queue.dma_start(out=bias_rows[row : row + FTILES, group, :], in_=given_bias[slot].rearrange("(m f) -> m f", f=P))
 
         new_loads(0)
         new_cells(0)
         new_loads(1)
-        for a in range(OP_SUM):
-            load_operand(0, a)
-        load_weight(H_SIDE * GATES + GATE_F)
-        load_weight(X_SIDE * GATES + GATE_F)
-        load_operand(0, OP_SUM)
-        for k in range(KIDS):
-            load_cell(0, k)
-        load_operand(1, OP_X)
-        for n, gate in enumerate((GATE_I, GATE_U, GATE_O)):
-            load_weight(H_SIDE * GATES + gate)
-            load_weight(X_SIDE * GATES + gate)
-            load_operand(1, OP_KID0 + n)
-        load_operand(1, OP_KID0 + 3)
-        load_operand(1, OP_SUM)
-        for slot in range(2 * GATES):
-            nc.gpsimd.dma_start(
-                out=bias_rows[slot * FTILES : (slot + 1) * FTILES, :],
-                in_=given_bias[slot].rearrange("(m f) -> m f", f=P),
-            )
+        load_bias(nc.scalar, 0, 0, X_SIDE * GATES + GATE_F)
+        load_bias(nc.scalar, 0, FTILES, H_SIDE * GATES + GATE_F)
+        gate_order = (GATE_F, GATE_I, GATE_U, GATE_O)
+        slots = [side * GATES + gate for gate in gate_order for side in (H_SIDE, X_SIDE)]
+        scale_jobs = [(slot, quadrant) for slot in slots for quadrant in range(4)]
+        large = (
+            [(load_operand, 0, OP_X), (load_operand, 0, OP_KID0), (load_weight, slots[0]), (load_weight, slots[1])]
+            + [(load_operand, 0, OP_KID0 + k) for k in range(1, KIDS)]
+            + [(load_cell, 0, k) for k in range(KIDS)]
+            + [(load_operand, 0, OP_SUM)]
+            + [(load_weight, slot) for slot in slots[2:]]
+            + [(load_operand, 1, a) for a in range(OPERANDS)]
+        )
+        for n, job in enumerate(large):
+            job[0](*job[1:])
+            for slot, quadrant in scale_jobs[2 * n : 2 * n + 2]:
+                load_scales(slot, quadrant)
+        for n, gate in enumerate(gate_order[1:]):
+            load_bias(nc.gpsimd, 1, n * FTILES, X_SIDE * GATES + gate)
+            load_bias(nc.gpsimd, 1, (3 + n) * FTILES, H_SIDE * GATES + gate)
 
         q_words = {}
         q_scales = {}
@@ -194,7 +198,7 @@ def tile_treelstm_pa_t_kernel(
 
         def squash(t, gate, func, z, out):
             m = t % FTILES
-            nc.scalar.activation(out=out, in_=z[:], func=func, bias=bias[:, gate, m : m + 1])
+            nc.scalar.activation(out=out, in_=z[:], func=func, bias=bias[:, gate_order.index(gate), m : m + 1])
 
         def transpose_cells(t, pair):
             b, m = divmod(t, FTILES)
@@ -217,24 +221,27 @@ def tile_treelstm_pa_t_kernel(
                 op=ALU.mult,
             )
 
-        def finish_cell(t):
-            iu = work.tile([P, BLOCK], F32, name="iu")
-            cell = work.tile([P, BLOCK], F32, name="cell")
-            nc.vector.tensor_tensor(out=iu[:], in0=live["gate_i", t][:], in1=live["gate_u", t][:], op=ALU.mult)
-            nc.vector.tensor_tensor(out=cell[:], in0=live["kid_sum", t][:], in1=iu[:], op=ALU.add)
-            live["cell", t] = cell
-
         def transpose_back(t, name):
             bank = tp_banks.tile([P, TILES, P], F32, name="back", tag="tp")
             for j in range(TILES):
                 nc.tensor.transpose(out=bank[:, j, :], in_=live[name, t][:, j * P : (j + 1) * P], identity=ident_f32[:])
             return bank
 
-        def store(t, bank, dram):
+        def store(t, node_major, dram):
             b, m = divmod(t, FTILES)
-            node_major = stores.tile([P, TILES, P], F32, name="node_major")
-            nc.scalar.copy(out=node_major[:], in_=bank[:])
             nc.sync.dma_start(out=dram[:, b * TILES : (b + 1) * TILES, m * P : (m + 1) * P], in_=node_major[:])
+
+        def spread_bias(group, first, gates):
+            width = gates * FTILES
+            bias_bank = tp_banks.tile([P, P], BF16, name="bias_bank", tag="tp")
+            nc.tensor.transpose(out=bias_bank[:], in_=bias_rows[:, group, :], identity=ident_bf16[:])
+            nc.vector.tensor_copy(out=bias_cols[:, :, 0:width], in_=bias_bank[:, 0 : 2 * width].rearrange("p (s c) -> p s c", s=2))
+            nc.vector.tensor_tensor(
+                out=bias[:, first : first + gates, :].rearrange("p g m -> p (g m)"),
+                in0=bias_cols[:, X_SIDE, 0:width],
+                in1=bias_cols[:, H_SIDE, 0:width],
+                op=ALU.add,
+            )
 
         waiting = None
         for count in range(AHEAD):
@@ -243,22 +250,25 @@ def tile_treelstm_pa_t_kernel(
             if waiting is not None:
                 quantise_unit(count - 1, waiting)
             waiting = grouped
+            if count == 1:
+                spread_bias(0, 0, 1)
         quantise_unit(AHEAD - 1, waiting)
 
-        bias_bank = tp_banks.tile([P, P], BF16, name="bias_bank", tag="tp")
-        nc.tensor.transpose(out=bias_bank[:], in_=bias_rows[:], identity=ident_bf16[:])
-        nc.vector.tensor_copy(out=bias_cols[:].rearrange("p s c -> p (s c)"), in_=bias_bank[:, 0 : 2 * GATES * FTILES])
-        nc.vector.tensor_tensor(
-            out=bias[:].rearrange("p g m -> p (g m)"), in0=bias_cols[:, X_SIDE, :], in1=bias_cols[:, H_SIDE, :], op=ALU.add
-        )
+        pending = None
 
-        for t in range(STEPS + 3):
+        def units_of_round(t):
+            if t == 0:
+                return list(range(AHEAD, UNITS))
+            if t < FTILES:
+                return list(range(UNITS + 4 * (t - 1), UNITS + 4 * t))
+            return [c for c in range(2 * UNITS + UNITS_PER_STEP * (t - FTILES), 2 * UNITS + UNITS_PER_STEP * (t - FTILES + 1)) if c < BLOCKS * UNITS]
+
+        for t in range(STEPS + 2):
             b, m = divmod(t, FTILES)
             has_f = t < STEPS
             has_g = 0 <= t - 1 < STEPS
-            has_c = 0 <= t - 2 < STEPS
-            has_s = 0 <= t - 3 < STEPS
-            counts = [c for c in range(AHEAD + t * UNITS_PER_STEP, AHEAD + (t + 1) * UNITS_PER_STEP) if c < BLOCKS * UNITS]
+            has_h = 0 <= t - 2 < STEPS
+            counts = units_of_round(t)
             if has_f and m == 1 and b + 1 < BLOCKS:
                 new_cells(b + 1)
                 for k in range(KIDS):
@@ -268,67 +278,74 @@ def tile_treelstm_pa_t_kernel(
                 for a in range(OPERANDS):
                     load_operand(b + 2, a)
 
+            jobs = []
+            if has_g:
+                for name, gate, func in (("gate_i", GATE_I, ACT.Sigmoid), ("gate_u", GATE_U, ACT.Tanh), ("gate_o", GATE_O, ACT.Sigmoid)):
+                    live[name, t - 1] = work.tile([P, BLOCK], F32, name=name)
+                    jobs.append((t - 1, gate, OP_SUM, func, live[name, t - 1][:]))
             if has_f:
                 live["forget", t] = work.tile([P, KIDS, BLOCK], F32, name="forget")
-                z_forget = [mx_group(t, GATE_F, OP_KID0 + k) for k in range(3)]
-            if has_s:
-                store(t - 3, live["back_c", t - 3], c_rows)
-                store(t - 3, live["back_h", t - 3], h_rows)
-            if has_c:
-                finish_cell(t - 2)
+                for k in range(KIDS):
+                    jobs.append((t, GATE_F, OP_KID0 + k, ACT.Sigmoid, live["forget", t][:, k, :]))
+            sums = []
+            for n in range(len(jobs) + 3):
+                if n >= 3:
+                    done = jobs[n - 3]
+                    squash(done[0], done[1], done[3], sums[n - 3], done[4])
+                if n < len(jobs):
+                    sums.append(mx_group(jobs[n][0], jobs[n][1], jobs[n][2]))
+
             if has_g:
-                live["kid_sum", t - 1] = work.tile([P, BLOCK], F32, name="kid_sum")
+                live["pair_sum", t - 1] = work.tile([P, 2, BLOCK], F32, name="pair_sum")
+                nc.vector.tensor_tensor(
+                    out=live["pair_sum", t - 1][:], in0=live["forget", t - 1][:, 0:2, :], in1=live["forget", t - 1][:, 2:4, :], op=ALU.add
+                )
+            if pending is not None:
+                quantise_unit(pending[0], pending[1])
+                pending = None
+            if has_g:
+                kid_sum = work.tile([P, BLOCK], F32, name="kid_sum")
                 pair_sum = live["pair_sum", t - 1]
-                nc.vector.tensor_tensor(out=live["kid_sum", t - 1][:], in0=pair_sum[:, 0, :], in1=pair_sum[:, 1, :], op=ALU.add)
-            if has_f:
-                for k in range(3):
-                    squash(t, GATE_F, ACT.Sigmoid, z_forget[k], live["forget", t][:, k, :])
-            xt = [transpose_unit(count) for count in counts[0:1]]
-            grouped = [regroup_unit(nc.scalar.copy, bank) for bank in xt]
+                nc.vector.tensor_tensor(out=kid_sum[:], in0=pair_sum[:, 0, :], in1=pair_sum[:, 1, :], op=ALU.add)
+                iu = work.tile([P, BLOCK], F32, name="iu")
+                nc.vector.tensor_tensor(out=iu[:], in0=live["gate_i", t - 1][:], in1=live["gate_u", t - 1][:], op=ALU.mult)
+            if has_h:
+                h_out = stores.tile([P, TILES, P], F32, name="h_out")
+                nc.vector.tensor_tensor(out=h_out[:], in0=live["tanh_c", t - 2][:], in1=live["back_o", t - 2][:], op=ALU.mult)
+                store(t - 2, h_out, h_rows)
+            if has_g:
+                live["cell", t - 1] = work.tile([P, BLOCK], F32, name="cell")
+                nc.vector.tensor_tensor(out=live["cell", t - 1][:], in0=kid_sum[:], in1=iu[:], op=ALU.add)
+
+            def prepare(n):
+                if n < len(counts):
+                    grouped = regroup_unit(nc.scalar.copy, transpose_unit(counts[n]))
+                    return (counts[n], grouped)
+                return None
+
             if t == 0:
-                transpose_cells(0, 0)
+                spread_bias(1, 1, 3)
+            first = prepare(0)
+            if has_f:
+                transpose_cells(t, 0)
+                products(t, 0)
+            if first is not None:
+                quantise_unit(first[0], first[1])
+            second = prepare(1)
             if has_f:
                 transpose_cells(t, 1)
-                products(t, 0)
-            for count, tile in zip(counts[0:1], grouped):
-                quantise_unit(count, tile)
-            if has_c:
-                tanh_c = work.tile([P, BLOCK], F32, name="tanh_c")
-                nc.scalar.activation(out=tanh_c[:], in_=live["cell", t - 2][:], func=ACT.Tanh)
-
-            if has_f:
-                z_last = mx_group(t, GATE_F, OP_KID0 + 3)
-            if has_g:
-                live["gate_i", t - 1] = work.tile([P, BLOCK], F32, name="gate_i")
-                z_i = mx_group(t - 1, GATE_I, OP_SUM)
-            xt = [transpose_unit(count) for count in counts[1:3]]
-            if has_f:
-                squash(t, GATE_F, ACT.Sigmoid, z_last, live["forget", t][:, 3, :])
-            if has_g:
-                squash(t - 1, GATE_I, ACT.Sigmoid, z_i, live["gate_i", t - 1][:])
-            grouped = [regroup_unit(nc.scalar.copy, bank) for bank in xt]
-            if has_c:
-                live["hid", t - 2] = work.tile([P, BLOCK], F32, name="hid")
-                nc.vector.tensor_tensor(out=live["hid", t - 2][:], in0=live["gate_o", t - 2][:], in1=tanh_c[:], op=ALU.mult)
-            if has_f:
                 products(t, 1)
-                live["pair_sum", t] = work.tile([P, 2, BLOCK], F32, name="pair_sum")
-                nc.vector.tensor_tensor(
-                    out=live["pair_sum", t][:], in0=live["forget", t][:, 0:2, :], in1=live["forget", t][:, 2:4, :], op=ALU.add
-                )
-            for count, tile in zip(counts[1:3], grouped):
-                quantise_unit(count, tile)
-
+            if second is not None:
+                quantise_unit(second[0], second[1])
+            for n in range(2, len(counts) - 1):
+                middle = prepare(n)
+                quantise_unit(middle[0], middle[1])
             if has_g:
-                live["gate_u", t - 1] = work.tile([P, BLOCK], F32, name="gate_u")
-                live["gate_o", t - 1] = work.tile([P, BLOCK], F32, name="gate_o")
-                z_u = mx_group(t - 1, GATE_U, OP_SUM)
-                z_o = mx_group(t - 1, GATE_O, OP_SUM)
-            if t + 1 < STEPS:
-                transpose_cells(t + 1, 0)
-            if has_c:
-                live["back_c", t - 2] = transpose_back(t - 2, "cell")
-                live["back_h", t - 2] = transpose_back(t - 2, "hid")
-            if has_g:
-                squash(t - 1, GATE_U, ACT.Tanh, z_u, live["gate_u", t - 1][:])
-                squash(t - 1, GATE_O, ACT.Sigmoid, z_o, live["gate_o", t - 1][:])
+                back_c = transpose_back(t - 1, "cell")
+                live["tanh_c", t - 1] = work.tile([P, TILES, P], F32, name="tanh_c")
+                nc.scalar.activation(out=live["tanh_c", t - 1][:], in_=back_c[:], func=ACT.Tanh)
+                c_out = stores.tile([P, TILES, P], F32, name="c_out")
+                nc.scalar.copy(out=c_out[:], in_=back_c[:])
+                store(t - 1, c_out, c_rows)
+                live["back_o", t - 1] = transpose_back(t - 1, "gate_o")
+            pending = prepare(len(counts) - 1) if len(counts) > 2 else None

@@ -205,10 +205,12 @@ def tile_treelstm_pa_t_kernel(
             bank = ct_banks.tile([P, 2, TILES, P], BF16, name="ct")
             for k in range(2):
                 for j in range(TILES):
-                    nc.tensor.transpose(
+                    nc.tensor.matmul(
                         out=bank[:, k, j, :],
-                        in_=cells[b][:, 2 * pair + k, j, m * P : (m + 1) * P],
-                        identity=ident_bf16[:],
+                        lhsT=cells[b][:, 2 * pair + k, j, m * P : (m + 1) * P],
+                        rhs=ident_bf16[:],
+                        start=True,
+                        stop=True,
                     )
             live["ct", t, pair] = bank
 
@@ -325,21 +327,22 @@ def tile_treelstm_pa_t_kernel(
 
             if t == 0:
                 spread_bias(1, 1, 3)
-            first = prepare(0)
             if has_f:
                 transpose_cells(t, 0)
                 products(t, 0)
+            first = prepare(0)
+            second = prepare(1)
             if first is not None:
                 quantise_unit(first[0], first[1])
-            second = prepare(1)
+            for n in range(2, len(counts) - 1):
+                middle = prepare(n)
+                quantise_unit(second[0], second[1])
+                second = middle
             if has_f:
                 transpose_cells(t, 1)
                 products(t, 1)
             if second is not None:
                 quantise_unit(second[0], second[1])
-            for n in range(2, len(counts) - 1):
-                middle = prepare(n)
-                quantise_unit(middle[0], middle[1])
             if has_g:
                 back_c = transpose_back(t - 1, "cell")
                 live["tanh_c", t - 1] = work.tile([P, TILES, P], F32, name="tanh_c")

@@ -67,9 +67,10 @@ def tile_treelstm_pa_t_kernel(
         quant = ctx.enter_context(tc.tile_pool(name="quant", bufs=3))
         work = ctx.enter_context(tc.tile_pool(name="work", bufs=2))
         stores = ctx.enter_context(tc.tile_pool(name="stores", bufs=4))
-        mx_banks = ctx.enter_context(tc.psum_pool(name="mx_banks", bufs=3))
-        ct_banks = ctx.enter_context(tc.psum_pool(name="ct_banks", bufs=2))
-        tp_banks = ctx.enter_context(tc.psum_pool(name="tp_banks", bufs=3))
+        banks = ctx.enter_context(tc.psum_pool(name="banks", bufs=8))
+        mx_banks = banks
+        ct_banks = banks
+        tp_banks = banks
         ctx.enter_context(tc.manual_schedule())
 
         w_words = const.tile([P, 2 * GATES, FEAT], U32, name="w_words", align_bytes=64)
@@ -152,7 +153,7 @@ def tile_treelstm_pa_t_kernel(
         def transpose_unit(count):
             b, unit = divmod(count, UNITS)
             a, half = divmod(unit, 2)
-            bank = tp_banks.tile([P, 2, 2, P], F32, name="xt", tag="tp")
+            bank = tp_banks.tile([P, 2, 2, P], F32, name="xt", tag="bank")
             for j in range(2):
                 row_words = operands[b][:, a, 2 * half + j, :].bitcast(F32)
                 for u in range(2):
@@ -182,7 +183,7 @@ def tile_treelstm_pa_t_kernel(
         def mx_group(t, gate, h_operand):
             b, m = divmod(t, FTILES)
             feats = slice(m * P, (m + 1) * P)
-            z = mx_banks.tile([P, BLOCK], F32, name="z")
+            z = mx_banks.tile([P, BLOCK], F32, name="z", tag="bank")
             for side, a in ((H_SIDE, h_operand), (X_SIDE, OP_X)):
                 slot = side * GATES + gate
                 nc.tensor.matmul_mx(
@@ -202,7 +203,7 @@ def tile_treelstm_pa_t_kernel(
 
         def transpose_cells(t, pair):
             b, m = divmod(t, FTILES)
-            bank = ct_banks.tile([P, 2, TILES, P], BF16, name="ct")
+            bank = ct_banks.tile([P, 2, TILES, P], BF16, name="ct", tag="bank")
             for k in range(2):
                 for j in range(TILES):
                     nc.tensor.matmul(
@@ -224,7 +225,7 @@ def tile_treelstm_pa_t_kernel(
             )
 
         def transpose_back(t, name):
-            bank = tp_banks.tile([P, TILES, P], F32, name="back", tag="tp")
+            bank = tp_banks.tile([P, TILES, P], F32, name="back", tag="bank")
             for j in range(TILES):
                 nc.tensor.transpose(out=bank[:, j, :], in_=live[name, t][:, j * P : (j + 1) * P], identity=ident_f32[:])
             return bank
@@ -235,7 +236,7 @@ def tile_treelstm_pa_t_kernel(
 
         def spread_bias(group, first, gates):
             width = gates * FTILES
-            bias_bank = tp_banks.tile([P, P], BF16, name="bias_bank", tag="tp")
+            bias_bank = tp_banks.tile([P, P], BF16, name="bias_bank", tag="bank")
             nc.tensor.transpose(out=bias_bank[:], in_=bias_rows[:, group, :], identity=ident_bf16[:])
             nc.vector.tensor_copy(out=bias_cols[:, :, 0:width], in_=bias_bank[:, 0 : 2 * width].rearrange("p (s c) -> p s c", s=2))
             nc.vector.tensor_tensor(

@@ -32,7 +32,7 @@ OPERANDS = 2 + KIDS
 HALF = BLOCK // 2
 UNITS = 2 * OPERANDS
 UNITS_PER_STEP = UNITS // FTILES
-AHEAD = 2 * OP_SUM
+AHEAD = UNITS
 
 FLOPS = 2 * FEAT * FEAT * (7 * NODES + KIDS * NODES)
 
@@ -128,10 +128,10 @@ def tile_treelstm_pa_t_kernel(
         slots = [side * GATES + gate for gate in gate_order for side in (H_SIDE, X_SIDE)]
         scale_jobs = [(slot, quadrant) for slot in slots for quadrant in range(4)]
         large = (
-            [(load_operand, 0, OP_X), (load_operand, 0, OP_KID0), (load_weight, slots[0]), (load_weight, slots[1])]
-            + [(load_operand, 0, OP_KID0 + k) for k in range(1, KIDS)]
-            + [(load_cell, 0, k) for k in range(KIDS)]
+            [(load_operand, 0, OP_X), (load_operand, 0, OP_KID0), (load_operand, 0, OP_KID0 + 1), (load_weight, slots[0]), (load_weight, slots[1])]
+            + [(load_operand, 0, OP_KID0 + k) for k in range(2, KIDS)]
             + [(load_operand, 0, OP_SUM)]
+            + [(load_cell, 0, k) for k in range(KIDS)]
             + [(load_weight, slot) for slot in slots[2:]]
             + [(load_operand, 1, a) for a in range(OPERANDS)]
         )
@@ -246,50 +246,25 @@ def tile_treelstm_pa_t_kernel(
                 op=ALU.add,
             )
 
-        waiting = None
-        for count in range(AHEAD):
-            bank = transpose_unit(count)
-            grouped = regroup_unit(nc.scalar.copy if count % 2 == 0 else nc.vector.tensor_copy, bank)
-            if waiting is not None:
-                quantise_unit(count - 1, waiting)
-            waiting = grouped
-            if count == 1:
-                spread_bias(0, 0, 1)
-        quantise_unit(AHEAD - 1, waiting)
+        lagging = []
 
-        pending = None
+        def flush():
+            for count, grouped in lagging:
+                quantise_unit(count, grouped)
+            lagging.clear()
 
-        def units_of_round(t):
-            if t == 0:
-                return list(range(AHEAD, UNITS))
-            if t < FTILES:
-                return list(range(UNITS + 4 * (t - 1), UNITS + 4 * t))
-            return [c for c in range(2 * UNITS + UNITS_PER_STEP * (t - FTILES), 2 * UNITS + UNITS_PER_STEP * (t - FTILES + 1)) if c < BLOCKS * UNITS]
+        def prepare(count, copy):
+            grouped = regroup_unit(copy, transpose_unit(count))
+            flush()
+            lagging.append((count, grouped))
 
-        for t in range(STEPS + 2):
-            b, m = divmod(t, FTILES)
-            has_f = t < STEPS
-            has_g = 0 <= t - 1 < STEPS
-            has_h = 0 <= t - 2 < STEPS
-            counts = units_of_round(t)
-            if has_f and m == 1 and b + 1 < BLOCKS:
-                new_cells(b + 1)
-                for k in range(KIDS):
-                    load_cell(b + 1, k)
-            if has_f and m == 1 and b + 2 < BLOCKS:
-                new_loads(b + 2)
-                for a in range(OPERANDS):
-                    load_operand(b + 2, a)
+        def new_forget(t):
+            live["forget", t] = work.tile([P, KIDS, BLOCK], F32, name="forget")
 
-            jobs = []
-            if has_g:
-                for name, gate, func in (("gate_i", GATE_I, ACT.Sigmoid), ("gate_u", GATE_U, ACT.Tanh), ("gate_o", GATE_O, ACT.Sigmoid)):
-                    live[name, t - 1] = work.tile([P, BLOCK], F32, name=name)
-                    jobs.append((t - 1, gate, OP_SUM, func, live[name, t - 1][:]))
-            if has_f:
-                live["forget", t] = work.tile([P, KIDS, BLOCK], F32, name="forget")
-                for k in range(KIDS):
-                    jobs.append((t, GATE_F, OP_KID0 + k, ACT.Sigmoid, live["forget", t][:, k, :]))
+        def forget_job(t, k):
+            return (t, GATE_F, OP_KID0 + k, ACT.Sigmoid, live["forget", t][:, k, :])
+
+        def run_jobs(jobs):
             sums = []
             for n in range(len(jobs) + 3):
                 if n >= 3:
@@ -298,58 +273,100 @@ def tile_treelstm_pa_t_kernel(
                 if n < len(jobs):
                     sums.append(mx_group(jobs[n][0], jobs[n][1], jobs[n][2]))
 
-            if has_g:
-                live["pair_sum", t - 1] = work.tile([P, 2, BLOCK], F32, name="pair_sum")
-                nc.vector.tensor_tensor(
-                    out=live["pair_sum", t - 1][:], in0=live["forget", t - 1][:, 0:2, :], in1=live["forget", t - 1][:, 2:4, :], op=ALU.add
-                )
-            if pending is not None:
-                quantise_unit(pending[0], pending[1])
-                pending = None
-            if has_g:
-                kid_sum = work.tile([P, BLOCK], F32, name="kid_sum")
-                pair_sum = live["pair_sum", t - 1]
-                nc.vector.tensor_tensor(out=kid_sum[:], in0=pair_sum[:, 0, :], in1=pair_sum[:, 1, :], op=ALU.add)
-                iu = work.tile([P, BLOCK], F32, name="iu")
-                nc.vector.tensor_tensor(out=iu[:], in0=live["gate_i", t - 1][:], in1=live["gate_u", t - 1][:], op=ALU.mult)
-            if has_h:
+        new_forget(0)
+        for count in range(AHEAD):
+            prepare(count, nc.scalar.copy if count % 2 == 0 else nc.vector.tensor_copy)
+            if count == 1:
+                spread_bias(0, 0, 1)
+            if count % 2 == 1 and count >= 5:
+                run_jobs([forget_job(0, (count - 5) // 2)])
+        flush()
+
+        def units_of_round(t):
+            if t < 2:
+                return []
+            if t < FTILES:
+                return list(range(UNITS + UNITS // 2 * (t - 2), UNITS + UNITS // 2 * (t - 1)))
+            first = 2 * UNITS + UNITS_PER_STEP * (t - FTILES)
+            return [c for c in range(first, first + UNITS_PER_STEP) if c < BLOCKS * UNITS]
+
+        def gate_steps(t):
+            if t == 1 or t == STEPS:
+                return []
+            return [s for s in range(0 if t == 2 else t - 1, t + 1 if t == STEPS - 1 else t) if 0 <= s < STEPS]
+
+        unfinished = []
+
+        def finish_hidden():
+            for s in unfinished:
                 h_out = stores.tile([P, TILES, P], F32, name="h_out")
-                nc.vector.tensor_tensor(out=h_out[:], in0=live["tanh_c", t - 2][:], in1=live["back_o", t - 2][:], op=ALU.mult)
-                store(t - 2, h_out, h_rows)
-            if has_g:
-                live["cell", t - 1] = work.tile([P, BLOCK], F32, name="cell")
-                nc.vector.tensor_tensor(out=live["cell", t - 1][:], in0=kid_sum[:], in1=iu[:], op=ALU.add)
+                nc.vector.tensor_tensor(out=h_out[:], in0=live["tanh_c", s][:], in1=live["back_o", s][:], op=ALU.mult)
+                store(s, h_out, h_rows)
+            unfinished.clear()
 
-            def prepare(n):
-                if n < len(counts):
-                    grouped = regroup_unit(nc.scalar.copy, transpose_unit(counts[n]))
-                    return (counts[n], grouped)
-                return None
+        for t in range(STEPS + 2):
+            b, m = divmod(t, FTILES)
+            has_f = t < STEPS
+            has_s = 0 <= t - 1 < STEPS
+            counts = units_of_round(t)
+            gated = gate_steps(t)
+            summed = [s for s in gated if s < t] + [s for s in (STEPS - 1,) if t == STEPS]
+            if has_f and m == 1 and b + 1 < BLOCKS:
+                new_cells(b + 1)
+                for k in range(KIDS):
+                    load_cell(b + 1, k)
+            if has_f and m == 2 and b + 2 < BLOCKS:
+                new_loads(b + 2)
+                for a in range(OPERANDS):
+                    load_operand(b + 2, a)
 
-            if t == 0:
+            if has_s:
+                pair_sum = work.tile([P, 2, BLOCK], F32, name="pair_sum")
+                nc.vector.tensor_tensor(out=pair_sum[:], in0=live["forget", t - 1][:, 0:2, :], in1=live["forget", t - 1][:, 2:4, :], op=ALU.add)
+            flush()
+            if has_s:
+                live["kid_sum", t - 1] = work.tile([P, BLOCK], F32, name="kid_sum")
+                nc.vector.tensor_tensor(out=live["kid_sum", t - 1][:], in0=pair_sum[:, 0, :], in1=pair_sum[:, 1, :], op=ALU.add)
+
+            jobs = []
+            for s in gated:
+                for name, gate, func in (("gate_i", GATE_I, ACT.Sigmoid), ("gate_u", GATE_U, ACT.Tanh), ("gate_o", GATE_O, ACT.Sigmoid)):
+                    live[name, s] = work.tile([P, BLOCK], F32, name=name)
+                    jobs.append((s, gate, OP_SUM, func, live[name, s][:]))
+            if has_f and t > 0:
+                new_forget(t)
+                jobs.extend([forget_job(t, k) for k in range(KIDS)])
+            run_jobs(jobs)
+
+            for s in gated:
+                live["iu", s] = work.tile([P, BLOCK], F32, name="iu")
+                nc.vector.tensor_tensor(out=live["iu", s][:], in0=live["gate_i", s][:], in1=live["gate_u", s][:], op=ALU.mult)
+            if t != STEPS:
+                finish_hidden()
+            for s in summed:
+                live["cell", s] = work.tile([P, BLOCK], F32, name="cell")
+                nc.vector.tensor_tensor(out=live["cell", s][:], in0=live["kid_sum", s][:], in1=live["iu", s][:], op=ALU.add)
+
+            if t == 1:
                 spread_bias(1, 1, 3)
+            split = (len(counts) + 1) // 2
             if has_f:
                 transpose_cells(t, 0)
                 products(t, 0)
-            first = prepare(0)
-            second = prepare(1)
-            if first is not None:
-                quantise_unit(first[0], first[1])
-            for n in range(2, len(counts) - 1):
-                middle = prepare(n)
-                quantise_unit(second[0], second[1])
-                second = middle
+            for count in counts[:split]:
+                prepare(count, nc.scalar.copy)
             if has_f:
                 transpose_cells(t, 1)
                 products(t, 1)
-            if second is not None:
-                quantise_unit(second[0], second[1])
-            if has_g:
-                back_c = transpose_back(t - 1, "cell")
-                live["tanh_c", t - 1] = work.tile([P, TILES, P], F32, name="tanh_c")
-                nc.scalar.activation(out=live["tanh_c", t - 1][:], in_=back_c[:], func=ACT.Tanh)
+            for s in summed:
+                finish_hidden()
+                back_c = transpose_back(s, "cell")
+                live["tanh_c", s] = work.tile([P, TILES, P], F32, name="tanh_c")
+                nc.scalar.activation(out=live["tanh_c", s][:], in_=back_c[:], func=ACT.Tanh)
                 c_out = stores.tile([P, TILES, P], F32, name="c_out")
                 nc.scalar.copy(out=c_out[:], in_=back_c[:])
-                store(t - 1, c_out, c_rows)
-                live["back_o", t - 1] = transpose_back(t - 1, "gate_o")
-            pending = prepare(len(counts) - 1) if len(counts) > 2 else None
+                store(s, c_out, c_rows)
+                live["back_o", s] = transpose_back(s, "gate_o")
+                unfinished.append(s)
+            for count in counts[split:]:
+                prepare(count, nc.scalar.copy)

@@ -291,9 +291,9 @@ def tile_treelstm_pa_t_kernel(
             return [c for c in range(first, first + UNITS_PER_STEP) if c < BLOCKS * UNITS]
 
         def gate_steps(t):
-            if t == 1 or t == STEPS:
+            if t == 1:
                 return []
-            return [s for s in range(0 if t == 2 else t - 1, t + 1 if t == STEPS - 1 else t) if 0 <= s < STEPS]
+            return [s for s in range(0 if t == 2 else t - 1, t) if s >= 0]
 
         unfinished = []
 
@@ -304,69 +304,95 @@ def tile_treelstm_pa_t_kernel(
                 store(s, h_out, h_rows)
             unfinished.clear()
 
-        for t in range(STEPS + 2):
+        def gate_jobs(s):
+            jobs = []
+            for name, gate, func in (("gate_i", GATE_I, ACT.Sigmoid), ("gate_u", GATE_U, ACT.Tanh), ("gate_o", GATE_O, ACT.Sigmoid)):
+                live[name, s] = work.tile([P, BLOCK], F32, name=name)
+                jobs.append((s, gate, OP_SUM, func, live[name, s][:]))
+            return jobs
+
+        def multiply_iu(s):
+            live["iu", s] = work.tile([P, BLOCK], F32, name="iu")
+            nc.vector.tensor_tensor(out=live["iu", s][:], in0=live["gate_i", s][:], in1=live["gate_u", s][:], op=ALU.mult)
+
+        def leave(s, pieces):
+            live["tanh_c", s] = work.tile([P, TILES, P], F32, name="tanh_c")
+            c_out = stores.tile([P, TILES, P], F32, name="c_out")
+            width = TILES // len(pieces)
+            for n, piece in enumerate(pieces):
+                nc.scalar.activation(out=live["tanh_c", s][:, n * width : (n + 1) * width, :], in_=piece, func=ACT.Tanh)
+            for n, piece in enumerate(pieces):
+                nc.scalar.copy(out=c_out[:, n * width : (n + 1) * width, :], in_=piece)
+            store(s, c_out, c_rows)
+            live["back_o", s] = transpose_back(s, "gate_o")
+            unfinished.append(s)
+
+        for t in range(STEPS):
             b, m = divmod(t, FTILES)
-            has_f = t < STEPS
-            has_s = 0 <= t - 1 < STEPS
             counts = units_of_round(t)
             gated = gate_steps(t)
-            summed = [s for s in gated if s < t] + [s for s in (STEPS - 1,) if t == STEPS]
-            if has_f and m == 1 and b + 1 < BLOCKS:
+            if m == 1 and b + 1 < BLOCKS:
                 new_cells(b + 1)
                 for k in range(KIDS):
                     load_cell(b + 1, k)
-            if has_f and m == 2 and b + 2 < BLOCKS:
+            if m == 2 and b + 2 < BLOCKS:
                 new_loads(b + 2)
                 for a in range(OPERANDS):
                     load_operand(b + 2, a)
 
-            if has_s:
+            if t > 0:
                 pair_sum = work.tile([P, 2, BLOCK], F32, name="pair_sum")
                 nc.vector.tensor_tensor(out=pair_sum[:], in0=live["forget", t - 1][:, 0:2, :], in1=live["forget", t - 1][:, 2:4, :], op=ALU.add)
             flush()
-            if has_s:
+            if t > 0:
                 live["kid_sum", t - 1] = work.tile([P, BLOCK], F32, name="kid_sum")
                 nc.vector.tensor_tensor(out=live["kid_sum", t - 1][:], in0=pair_sum[:, 0, :], in1=pair_sum[:, 1, :], op=ALU.add)
 
             jobs = []
             for s in gated:
-                for name, gate, func in (("gate_i", GATE_I, ACT.Sigmoid), ("gate_u", GATE_U, ACT.Tanh), ("gate_o", GATE_O, ACT.Sigmoid)):
-                    live[name, s] = work.tile([P, BLOCK], F32, name=name)
-                    jobs.append((s, gate, OP_SUM, func, live[name, s][:]))
-            if has_f and t > 0:
+                jobs.extend(gate_jobs(s))
+            if t > 0:
                 new_forget(t)
                 jobs.extend([forget_job(t, k) for k in range(KIDS)])
             run_jobs(jobs)
 
             for s in gated:
-                live["iu", s] = work.tile([P, BLOCK], F32, name="iu")
-                nc.vector.tensor_tensor(out=live["iu", s][:], in0=live["gate_i", s][:], in1=live["gate_u", s][:], op=ALU.mult)
-            if t != STEPS:
-                finish_hidden()
-            for s in summed:
+                multiply_iu(s)
+            finish_hidden()
+            for s in gated:
                 live["cell", s] = work.tile([P, BLOCK], F32, name="cell")
                 nc.vector.tensor_tensor(out=live["cell", s][:], in0=live["kid_sum", s][:], in1=live["iu", s][:], op=ALU.add)
 
             if t == 1:
                 spread_bias(1, 1, 3)
             split = (len(counts) + 1) // 2
-            if has_f:
-                transpose_cells(t, 0)
-                products(t, 0)
+            transpose_cells(t, 0)
+            products(t, 0)
             for count in counts[:split]:
                 prepare(count, nc.scalar.copy)
-            if has_f:
-                transpose_cells(t, 1)
-                products(t, 1)
-            for s in summed:
+            transpose_cells(t, 1)
+            products(t, 1)
+            if t == STEPS - 1:
+                run_jobs(gate_jobs(t))
+            for s in gated:
                 finish_hidden()
-                back_c = transpose_back(s, "cell")
-                live["tanh_c", s] = work.tile([P, TILES, P], F32, name="tanh_c")
-                nc.scalar.activation(out=live["tanh_c", s][:], in_=back_c[:], func=ACT.Tanh)
-                c_out = stores.tile([P, TILES, P], F32, name="c_out")
-                nc.scalar.copy(out=c_out[:], in_=back_c[:])
-                store(s, c_out, c_rows)
-                live["back_o", s] = transpose_back(s, "gate_o")
-                unfinished.append(s)
+                leave(s, [transpose_back(s, "cell")[:]])
             for count in counts[split:]:
                 prepare(count, nc.scalar.copy)
+
+        last = STEPS - 1
+        parts = [live["forget", last][:, k, :] for k in range(KIDS)]
+        multiply_iu(last)
+        parts.append(live["iu", last][:])
+        pieces = []
+        for j in range(TILES):
+            piece = banks.tile([P, 1, P], F32, name="piece", tag="bank")
+            pieces.append(piece)
+        for n, part in enumerate(parts):
+            for j in range(TILES):
+                nc.tensor.matmul(
+                    out=pieces[j][:, 0, :], lhsT=part[:, j * P : (j + 1) * P], rhs=ident_f32[:], is_transpose=True, start=(n == 0), stop=(n == len(parts) - 1)
+                )
+        finish_hidden()
+        leave(last, [piece[:] for piece in pieces])
+        finish_hidden()

@@ -64,6 +64,7 @@ def tile_treelstm_pa_t_kernel(
         const = ctx.enter_context(tc.tile_pool(name="const", bufs=1))
         loads = ctx.enter_context(tc.tile_pool(name="loads", bufs=2))
         regroup = ctx.enter_context(tc.tile_pool(name="regroup", bufs=4))
+        sorting = ctx.enter_context(tc.tile_pool(name="sorting", bufs=4))
         quant = ctx.enter_context(tc.tile_pool(name="quant", bufs=3))
         work = ctx.enter_context(tc.tile_pool(name="work", bufs=2))
         stores = ctx.enter_context(tc.tile_pool(name="stores", bufs=4))
@@ -150,6 +151,15 @@ def tile_treelstm_pa_t_kernel(
             q_words[b] = quant.tile([P, OPERANDS, BLOCK], U32, name="q_words", align_bytes=64)
             q_scales[b] = quant.tile([P, OPERANDS, BLOCK], U8, name="q_scales", align_bytes=64)
 
+        sorted_words = {}
+
+        def sort_unit(count):
+            b, unit = divmod(count, UNITS)
+            a, half = divmod(unit, 2)
+            sorted_words[count] = sorting.tile([P, 2, 2, P], F32, name="sorted_words")
+            rows = operands[b][:, a, 2 * half : 2 * half + 2, :].bitcast(F32)
+            nc.vector.tensor_copy(out=sorted_words[count][:], in_=rows.rearrange("n j (p u) -> n j u p", u=2))
+
         def transpose_unit(count):
             b, unit = divmod(count, UNITS)
             a, half = divmod(unit, 2)
@@ -157,7 +167,8 @@ def tile_treelstm_pa_t_kernel(
             for j in range(2):
                 row_words = operands[b][:, a, 2 * half + j, :].bitcast(F32)
                 for u in range(2):
-                    nc.tensor.transpose(out=bank[:, j, u, :], in_=row_words[:, u:WORDS:2], identity=ident_f32[:])
+                    words = sorted_words[count][:, j, u, :] if count in sorted_words else row_words[:, u:WORDS:2]
+                    nc.tensor.transpose(out=bank[:, j, u, :], in_=words, identity=ident_f32[:])
             return bank
 
         def regroup_unit(copy, bank):
@@ -362,6 +373,10 @@ def tile_treelstm_pa_t_kernel(
             for s in gated:
                 live["cell", s] = work.tile([P, BLOCK], F32, name="cell")
                 nc.vector.tensor_tensor(out=live["cell", s][:], in0=live["kid_sum", s][:], in1=live["iu", s][:], op=ALU.add)
+
+            if t >= 2:
+                for count in units_of_round(t + 1)[0:2]:
+                    sort_unit(count)
 
             if t == 1:
                 spread_bias(1, 1, 3)

@@ -64,7 +64,7 @@ def tile_treelstm_pa_t_kernel(
         const = ctx.enter_context(tc.tile_pool(name="const", bufs=1))
         loads = ctx.enter_context(tc.tile_pool(name="loads", bufs=2))
         regroup = ctx.enter_context(tc.tile_pool(name="regroup", bufs=4))
-        sorting = ctx.enter_context(tc.tile_pool(name="sorting", bufs=4))
+        sorting = ctx.enter_context(tc.tile_pool(name="sorting", bufs=2))
         quant = ctx.enter_context(tc.tile_pool(name="quant", bufs=3))
         work = ctx.enter_context(tc.tile_pool(name="work", bufs=2))
         stores = ctx.enter_context(tc.tile_pool(name="stores", bufs=4))
@@ -153,12 +153,12 @@ def tile_treelstm_pa_t_kernel(
 
         sorted_words = {}
 
-        def sort_unit(count):
+        def sort_operand(count):
             b, unit = divmod(count, UNITS)
-            a, half = divmod(unit, 2)
-            sorted_words[count] = sorting.tile([P, 2, 2, P], F32, name="sorted_words")
-            rows = operands[b][:, a, 2 * half : 2 * half + 2, :].bitcast(F32)
-            nc.vector.tensor_copy(out=sorted_words[count][:], in_=rows.rearrange("n j (p u) -> n j u p", u=2))
+            words = sorting.tile([P, TILES, 2, P], F32, name="words")
+            nc.vector.tensor_copy(out=words[:], in_=operands[b][:, unit // 2, :, :].bitcast(F32).rearrange("n j (p u) -> n j u p", u=2))
+            for half in range(2):
+                sorted_words[count + half] = words[:, 2 * half : 2 * half + 2, :, :]
 
         def transpose_unit(count):
             b, unit = divmod(count, UNITS)
@@ -351,13 +351,23 @@ def tile_treelstm_pa_t_kernel(
                 for a in range(OPERANDS):
                     load_operand(b + 2, a)
 
+            bare = t > 0 and not lagging
             if t > 0:
                 pair_sum = work.tile([P, 2, BLOCK], F32, name="pair_sum")
-                nc.vector.tensor_tensor(out=pair_sum[:], in0=live["forget", t - 1][:, 0:2, :], in1=live["forget", t - 1][:, 2:4, :], op=ALU.add)
+                products_of = live["forget", t - 1]
+                if bare:
+                    for pair in range(2):
+                        nc.vector.tensor_tensor(out=pair_sum[:, pair, :], in0=products_of[:, 2 * pair, :], in1=products_of[:, 2 * pair + 1, :], op=ALU.add)
+                else:
+                    nc.vector.tensor_tensor(out=pair_sum[:], in0=products_of[:, 0:2, :], in1=products_of[:, 2:4, :], op=ALU.add)
             flush()
-            if t > 0:
+
+            def add_pairs():
                 live["kid_sum", t - 1] = work.tile([P, BLOCK], F32, name="kid_sum")
                 nc.vector.tensor_tensor(out=live["kid_sum", t - 1][:], in0=pair_sum[:, 0, :], in1=pair_sum[:, 1, :], op=ALU.add)
+
+            if t > 0 and not bare:
+                add_pairs()
 
             jobs = []
             for s in gated:
@@ -369,17 +379,19 @@ def tile_treelstm_pa_t_kernel(
 
             for s in gated:
                 multiply_iu(s)
+            if t == 1:
+                spread_bias(1, 1, 3)
+            if bare:
+                add_pairs()
             finish_hidden()
             for s in gated:
                 live["cell", s] = work.tile([P, BLOCK], F32, name="cell")
                 nc.vector.tensor_tensor(out=live["cell", s][:], in0=live["kid_sum", s][:], in1=live["iu", s][:], op=ALU.add)
 
             if t >= 2:
-                for count in units_of_round(t + 1)[0:2]:
-                    sort_unit(count)
+                for count in [c for c in units_of_round(t + 1) if c % 2 == 0 and c + 1 in units_of_round(t + 1)][0:1]:
+                    sort_operand(count)
 
-            if t == 1:
-                spread_bias(1, 1, 3)
             split = (len(counts) + 1) // 2
             transpose_cells(t, 0)
             products(t, 0)

@@ -393,12 +393,17 @@ def tile_treelstm_pa_t_kernel(
                     sort_operand(count)
 
             split = (len(counts) + 1) // 2
+            one_run = len(counts) == UNITS_PER_STEP
             transpose_cells(t, 0)
             products(t, 0)
+            if one_run:
+                transpose_cells(t, 1)
+                products(t, 1)
             for count in counts[:split]:
                 prepare(count, nc.scalar.copy)
-            transpose_cells(t, 1)
-            products(t, 1)
+            if not one_run:
+                transpose_cells(t, 1)
+                products(t, 1)
             if t == STEPS - 1:
                 run_jobs(gate_jobs(t))
             for s in gated:

@@ -83,9 +83,11 @@ def tile_treelstm_pa_t_kernel(
         bias = const.tile([P, GATES, FTILES], F32, name="bias")
         warm = const.tile([P, 2], F32, name="warm")
 
-        nc.vector.memset(w_scales[:].bitcast(I32), 0)
-        nc.vector.memset(bias_rows[:], 0.0)
         nc.vector.memset(warm[:], 0.0)
+        nc.vector.memset(bias_rows[:], 0.0)
+        nc.vector.memset(w_scales[:].bitcast(I32), 0)
+        for row, vector in ((0, b_fx), (FTILES, b_fh)):
+            nc.scalar.dma_start(out=bias_rows[row : row + FTILES, 0, :], in_=vector.rearrange("(m f) -> m f", f=P))
         nc.scalar.activation(out=warm[:, 1:2], in_=warm[:, 0:1], func=ACT.Sigmoid)
         make_identity(nc, ident_f32[:])
         nc.scalar.copy(out=ident_bf16[:], in_=ident_f32[:])
@@ -123,8 +125,6 @@ def tile_treelstm_pa_t_kernel(
         new_loads(0)
         new_cells(0)
         new_loads(1)
-        load_bias(nc.scalar, 0, 0, X_SIDE * GATES + GATE_F)
-        load_bias(nc.scalar, 0, FTILES, H_SIDE * GATES + GATE_F)
         gate_order = (GATE_F, GATE_I, GATE_U, GATE_O)
         slots = [side * GATES + gate for gate in gate_order for side in (H_SIDE, X_SIDE)]
         scale_jobs = [(slot, quadrant) for slot in slots for quadrant in range(4)]

@@ -67,6 +67,7 @@ def tile_treelstm_pa_t_kernel(
         sorting = ctx.enter_context(tc.tile_pool(name="sorting", bufs=2))
         quant = ctx.enter_context(tc.tile_pool(name="quant", bufs=3))
         work = ctx.enter_context(tc.tile_pool(name="work", bufs=2))
+        turn = ctx.enter_context(tc.tile_pool(name="turn", bufs=1))
         stores = ctx.enter_context(tc.tile_pool(name="stores", bufs=4))
         banks = ctx.enter_context(tc.psum_pool(name="banks", bufs=8))
         mx_banks = banks
@@ -94,6 +95,10 @@ def tile_treelstm_pa_t_kernel(
 
         operands = {}
         cells = {}
+
+        def prep_order(b):
+            kids = [OP_KID0 + k for k in range(KIDS)]
+            return [OP_X] + kids + [OP_SUM] if b == 0 else [OP_X, OP_SUM] + kids
 
         def new_loads(b):
             operands[b] = loads.tile([P, OPERANDS, TILES, FEAT], BF16, name="operands")
@@ -134,7 +139,7 @@ def tile_treelstm_pa_t_kernel(
             + [(load_operand, 0, OP_SUM)]
             + [(load_cell, 0, k) for k in range(KIDS)]
             + [(load_weight, slot) for slot in slots[2:]]
-            + [(load_operand, 1, a) for a in range(OPERANDS)]
+            + [(load_operand, 1, a) for a in prep_order(1)]
         )
         for n, job in enumerate(large):
             job[0](*job[1:])
@@ -153,16 +158,18 @@ def tile_treelstm_pa_t_kernel(
 
         sorted_words = {}
 
-        def sort_operand(count):
+        def sort_units(count, units):
             b, unit = divmod(count, UNITS)
-            words = sorting.tile([P, TILES, 2, P], F32, name="words")
-            nc.vector.tensor_copy(out=words[:], in_=operands[b][:, unit // 2, :, :].bitcast(F32).rearrange("n j (p u) -> n j u p", u=2))
-            for half in range(2):
-                sorted_words[count + half] = words[:, 2 * half : 2 * half + 2, :, :]
+            first_row = 2 * (unit % 2)
+            words = sorting.tile([P, 2 * units, 2, P], F32, name="words" if units == 2 else "half_words")
+            rows = operands[b][:, prep_order(b)[unit // 2], first_row : first_row + 2 * units, :]
+            nc.vector.tensor_copy(out=words[:], in_=rows.bitcast(F32).rearrange("n j (p u) -> n j u p", u=2))
+            for n in range(units):
+                sorted_words[count + n] = words[:, 2 * n : 2 * n + 2, :, :]
 
         def transpose_unit(count):
             b, unit = divmod(count, UNITS)
-            a, half = divmod(unit, 2)
+            a, half = prep_order(b)[unit // 2], unit % 2
             bank = tp_banks.tile([P, 2, 2, P], F32, name="xt", tag="bank")
             for j in range(2):
                 row_words = operands[b][:, a, 2 * half + j, :].bitcast(F32)
@@ -179,7 +186,7 @@ def tile_treelstm_pa_t_kernel(
 
         def quantise_unit(count, grouped):
             b, unit = divmod(count, UNITS)
-            a, half = divmod(unit, 2)
+            a, half = prep_order(b)[unit // 2], unit % 2
             if unit == 0:
                 new_quantised(b)
             cols = slice(half * HALF, (half + 1) * HALF)
@@ -302,9 +309,16 @@ def tile_treelstm_pa_t_kernel(
             return [c for c in range(first, first + UNITS_PER_STEP) if c < BLOCKS * UNITS]
 
         def gate_steps(t):
-            if t == 1:
+            if t < 2 or t == STEPS - 1:
                 return []
-            return [s for s in range(0 if t == 2 else t - 1, t) if s >= 0]
+            if t < FTILES:
+                return [2 * (t - 2), 2 * (t - 2) + 1]
+            return [t]
+
+        def finish_steps(t):
+            if t < 2:
+                return []
+            return [0, 1] if t == 2 else [t - 1]
 
         unfinished = []
 
@@ -322,9 +336,13 @@ def tile_treelstm_pa_t_kernel(
                 jobs.append((s, gate, OP_SUM, func, live[name, s][:]))
             return jobs
 
-        def multiply_iu(s):
-            live["iu", s] = work.tile([P, BLOCK], F32, name="iu")
-            nc.vector.tensor_tensor(out=live["iu", s][:], in0=live["gate_i", s][:], in1=live["gate_u", s][:], op=ALU.mult)
+        def multiply_iu(s, engine, pool):
+            live["iu", s] = pool.tile([P, BLOCK], F32, name="iu")
+            engine.tensor_tensor(out=live["iu", s][:], in0=live["gate_i", s][:], in1=live["gate_u", s][:], op=ALU.mult)
+
+        def add_pair(s, name, engine, first):
+            live[name, s] = work.tile([P, BLOCK], F32, name=name)
+            engine.tensor_tensor(out=live[name, s][:], in0=live["forget", s][:, first, :], in1=live["forget", s][:, first + 1, :], op=ALU.add)
 
         def leave(s, pieces):
             live["tanh_c", s] = work.tile([P, TILES, P], F32, name="tanh_c")
@@ -342,32 +360,19 @@ def tile_treelstm_pa_t_kernel(
             b, m = divmod(t, FTILES)
             counts = units_of_round(t)
             gated = gate_steps(t)
+            finished = finish_steps(t)
             if m == 1 and b + 1 < BLOCKS:
                 new_cells(b + 1)
                 for k in range(KIDS):
                     load_cell(b + 1, k)
             if m == 2 and b + 2 < BLOCKS:
                 new_loads(b + 2)
-                for a in range(OPERANDS):
+                for a in prep_order(b + 2):
                     load_operand(b + 2, a)
 
-            bare = t > 0 and not lagging
             if t > 0:
-                pair_sum = work.tile([P, 2, BLOCK], F32, name="pair_sum")
-                products_of = live["forget", t - 1]
-                if bare:
-                    for pair in range(2):
-                        nc.vector.tensor_tensor(out=pair_sum[:, pair, :], in0=products_of[:, 2 * pair, :], in1=products_of[:, 2 * pair + 1, :], op=ALU.add)
-                else:
-                    nc.vector.tensor_tensor(out=pair_sum[:], in0=products_of[:, 0:2, :], in1=products_of[:, 2:4, :], op=ALU.add)
+                add_pair(t - 1, "late_pair", nc.vector, 2)
             flush()
-
-            def add_pairs():
-                live["kid_sum", t - 1] = work.tile([P, BLOCK], F32, name="kid_sum")
-                nc.vector.tensor_tensor(out=live["kid_sum", t - 1][:], in0=pair_sum[:, 0, :], in1=pair_sum[:, 1, :], op=ALU.add)
-
-            if t > 0 and not bare:
-                add_pairs()
 
             jobs = []
             for s in gated:
@@ -377,25 +382,36 @@ def tile_treelstm_pa_t_kernel(
                 jobs.extend([forget_job(t, k) for k in range(KIDS)])
             run_jobs(jobs)
 
-            for s in gated:
-                multiply_iu(s)
+            for s in finished:
+                if ("iu", s) not in live:
+                    multiply_iu(s, nc.vector, work)
             if t == 1:
                 spread_bias(1, 1, 3)
-            if bare:
-                add_pairs()
+            coming = units_of_round(t + 1) if t >= 2 else []
+            to_sort = [c for c in coming if c % 2 == 0 and c + 1 in coming][0:1]
+            if len(coming) == UNITS_PER_STEP:
+                for count in [c for c in coming if c not in (to_sort[0], to_sort[0] + 1)]:
+                    sort_units(count, 1)
+            for s in finished:
+                nc.vector.tensor_tensor(out=live["iu", s][:], in0=live["iu", s][:], in1=live["early_pair", s][:], op=ALU.add)
+            for count in to_sort:
+                sort_units(count, 2)
+            if not to_sort:
+                finish_hidden()
+            for s in finished:
+                live["cell", s] = work.tile([P, BLOCK], F32, name="cell")
+                nc.vector.tensor_tensor(out=live["cell", s][:], in0=live["late_pair", s][:], in1=live["iu", s][:], op=ALU.add)
             finish_hidden()
             for s in gated:
-                live["cell", s] = work.tile([P, BLOCK], F32, name="cell")
-                nc.vector.tensor_tensor(out=live["cell", s][:], in0=live["kid_sum", s][:], in1=live["iu", s][:], op=ALU.add)
-
-            if t >= 2:
-                for count in [c for c in units_of_round(t + 1) if c % 2 == 0 and c + 1 in units_of_round(t + 1)][0:1]:
-                    sort_operand(count)
+                if s not in finished:
+                    multiply_iu(s, nc.gpsimd, turn)
 
             split = (len(counts) + 1) // 2
             one_run = len(counts) == UNITS_PER_STEP
             transpose_cells(t, 0)
             products(t, 0)
+            if t < STEPS - 1:
+                add_pair(t, "early_pair", nc.gpsimd, 0)
             if one_run:
                 transpose_cells(t, 1)
                 products(t, 1)
@@ -406,7 +422,7 @@ def tile_treelstm_pa_t_kernel(
                 products(t, 1)
             if t == STEPS - 1:
                 run_jobs(gate_jobs(t))
-            for s in gated:
+            for s in finished:
                 finish_hidden()
                 leave(s, [transpose_back(s, "cell")[:]])
             for count in counts[split:]:
@@ -414,7 +430,7 @@ def tile_treelstm_pa_t_kernel(
 
         last = STEPS - 1
         parts = [live["forget", last][:, k, :] for k in range(KIDS)]
-        multiply_iu(last)
+        multiply_iu(last, nc.vector, work)
         parts.append(live["iu", last][:])
         pieces = []
         for j in range(TILES):

@@ -65,7 +65,7 @@ def tile_treelstm_pa_t_kernel(
         loads = ctx.enter_context(tc.tile_pool(name="loads", bufs=2))
         regroup = ctx.enter_context(tc.tile_pool(name="regroup", bufs=4))
         sorting = ctx.enter_context(tc.tile_pool(name="sorting", bufs=2))
-        quant = ctx.enter_context(tc.tile_pool(name="quant", bufs=3))
+        quant = ctx.enter_context(tc.tile_pool(name="quant", bufs=2))
         work = ctx.enter_context(tc.tile_pool(name="work", bufs=2))
         turn = ctx.enter_context(tc.tile_pool(name="turn", bufs=1))
         stores = ctx.enter_context(tc.tile_pool(name="stores", bufs=4))
@@ -161,7 +161,10 @@ def tile_treelstm_pa_t_kernel(
         def sort_units(count, units):
             b, unit = divmod(count, UNITS)
             first_row = 2 * (unit % 2)
-            words = sorting.tile([P, 2 * units, 2, P], F32, name="words" if units == 2 else "half_words")
+            if units == 2:
+                words = sorting.tile([P, 2 * units, 2, P], F32, name="words", bufs=6)
+            else:
+                words = sorting.tile([P, 2 * units, 2, P], F32, name="half_words")
             rows = operands[b][:, prep_order(b)[unit // 2], first_row : first_row + 2 * units, :]
             nc.vector.tensor_copy(out=words[:], in_=rows.bitcast(F32).rearrange("n j (p u) -> n j u p", u=2))
             for n in range(units):
@@ -387,16 +390,17 @@ def tile_treelstm_pa_t_kernel(
                     multiply_iu(s, nc.vector, work)
             if t == 1:
                 spread_bias(1, 1, 3)
-            coming = units_of_round(t + 1) if t >= 2 else []
-            to_sort = [c for c in coming if c % 2 == 0 and c + 1 in coming][0:1]
-            if len(coming) == UNITS_PER_STEP:
-                for count in [c for c in coming if c not in (to_sort[0], to_sort[0] + 1)]:
-                    sort_units(count, 1)
+            coming = units_of_round(t + 1)
+            to_sort = [c for c in coming if c % 2 == 0 and c + 1 in coming]
+            for count in [c for c in coming if c not in to_sort and c - 1 not in to_sort]:
+                sort_units(count, 1)
             for s in finished:
                 nc.vector.tensor_tensor(out=live["iu", s][:], in0=live["iu", s][:], in1=live["early_pair", s][:], op=ALU.add)
-            for count in to_sort:
-                sort_units(count, 2)
-            if not to_sort:
+            late_data = t + 1 < FTILES
+            if not late_data:
+                for count in to_sort:
+                    sort_units(count, 2)
+            if late_data or not to_sort:
                 finish_hidden()
             for s in finished:
                 live["cell", s] = work.tile([P, BLOCK], F32, name="cell")
@@ -427,6 +431,9 @@ def tile_treelstm_pa_t_kernel(
                 leave(s, [transpose_back(s, "cell")[:]])
             for count in counts[split:]:
                 prepare(count, nc.scalar.copy)
+            if late_data:
+                for count in to_sort:
+                    sort_units(count, 2)
 
         last = STEPS - 1
         parts = [live["forget", last][:, k, :] for k in range(KIDS)]

@@ -83,10 +83,16 @@ def tile_treelstm_pa_t_kernel(
         bias_cols = const.tile([P, 2, GATES * FTILES], F32, name="bias_cols")
         bias = const.tile([P, GATES, FTILES], F32, name="bias")
         warm = const.tile([P, 2], F32, name="warm")
+        ones = const.tile([P, P], BF16, name="ones")
+        o_bias_rows = const.tile([P, FEAT], BF16, name="o_bias_rows")
+        o_bias = const.tile([P, FEAT], F32, name="o_bias")
+        o_last = const.tile([P, TILES, FEAT], F32, name="o_last")
 
         nc.vector.memset(warm[:], 0.0)
         nc.vector.memset(bias_rows[:], 0.0)
         nc.vector.memset(w_scales[:].bitcast(I32), 0)
+        nc.vector.memset(ones[:], 1.0)
+        nc.vector.memset(o_bias_rows[:], 0.0)
         for row, vector in ((0, b_fx), (FTILES, b_fh)):
             nc.scalar.dma_start(out=bias_rows[row : row + FTILES, 0, :], in_=vector.rearrange("(m f) -> m f", f=P))
         nc.scalar.activation(out=warm[:, 1:2], in_=warm[:, 0:1], func=ACT.Sigmoid)
@@ -148,6 +154,8 @@ def tile_treelstm_pa_t_kernel(
         for n, gate in enumerate(gate_order[1:]):
             load_bias(nc.gpsimd, 1, n * FTILES, X_SIDE * GATES + gate)
             load_bias(nc.gpsimd, 1, (3 + n) * FTILES, H_SIDE * GATES + gate)
+        for row, vector in enumerate((b_ox, b_oh)):
+            nc.gpsimd.dma_start(out=o_bias_rows[row : row + 1, :], in_=vector.rearrange("(o f) -> o f", o=1))
 
         q_words = {}
         q_scales = {}
@@ -162,7 +170,7 @@ def tile_treelstm_pa_t_kernel(
             b, unit = divmod(count, UNITS)
             first_row = 2 * (unit % 2)
             if units == 2:
-                words = sorting.tile([P, 2 * units, 2, P], F32, name="words", bufs=6)
+                words = sorting.tile([P, 2 * units, 2, P], F32, name="words", bufs=4)
             else:
                 words = sorting.tile([P, 2 * units, 2, P], F32, name="half_words")
             rows = operands[b][:, prep_order(b)[unit // 2], first_row : first_row + 2 * units, :]
@@ -216,6 +224,23 @@ def tile_treelstm_pa_t_kernel(
                     start=(side == H_SIDE),
                     stop=(side == X_SIDE),
                 )
+            return z
+
+        def o_group(j):
+            nodes = slice(j * P, (j + 1) * P)
+            z = banks.tile([P, FEAT], F32, name="z_o", tag="bank")
+            for side, a in ((H_SIDE, OP_SUM), (X_SIDE, OP_X)):
+                slot = side * GATES + GATE_O
+                nc.tensor.matmul_mx(
+                    out=z[:],
+                    lhsT=q_words[BLOCKS - 1][:, a, nodes].bitcast(FP8X4),
+                    lhsT_scale=q_scales[BLOCKS - 1][:, a, nodes],
+                    rhs=w_words[:, slot, :].bitcast(FP8X4),
+                    rhs_scale=w_scales[:, slot, :],
+                    start=(side == H_SIDE),
+                    stop=(side == X_SIDE),
+                )
+            live["z_o", j] = z
             return z
 
         def squash(t, gate, func, z, out):
@@ -288,11 +313,11 @@ def tile_treelstm_pa_t_kernel(
         def run_jobs(jobs):
             sums = []
             for n in range(len(jobs) + 3):
-                if n >= 3:
+                if n >= 3 and len(jobs[n - 3]) > 1:
                     done = jobs[n - 3]
                     squash(done[0], done[1], done[3], sums[n - 3], done[4])
                 if n < len(jobs):
-                    sums.append(mx_group(jobs[n][0], jobs[n][1], jobs[n][2]))
+                    sums.append(mx_group(jobs[n][0], jobs[n][1], jobs[n][2]) if len(jobs[n]) > 1 else o_group(jobs[n][0]))
 
         new_forget(0)
         for count in range(AHEAD):
@@ -328,13 +353,17 @@ def tile_treelstm_pa_t_kernel(
         def finish_hidden():
             for s in unfinished:
                 h_out = stores.tile([P, TILES, P], F32, name="h_out")
-                nc.vector.tensor_tensor(out=h_out[:], in0=live["tanh_c", s][:], in1=live["back_o", s][:], op=ALU.mult)
+                o_gate = live["back_o", s][:] if ("back_o", s) in live else o_last[:, :, (s % FTILES) * P : (s % FTILES + 1) * P]
+                nc.vector.tensor_tensor(out=h_out[:], in0=live["tanh_c", s][:], in1=o_gate, op=ALU.mult)
                 store(s, h_out, h_rows)
             unfinished.clear()
 
         def gate_jobs(s):
             jobs = []
-            for name, gate, func in (("gate_i", GATE_I, ACT.Sigmoid), ("gate_u", GATE_U, ACT.Tanh), ("gate_o", GATE_O, ACT.Sigmoid)):
+            gates = [("gate_i", GATE_I, ACT.Sigmoid), ("gate_u", GATE_U, ACT.Tanh)]
+            if s // FTILES < BLOCKS - 1:
+                gates.append(("gate_o", GATE_O, ACT.Sigmoid))
+            for name, gate, func in gates:
                 live[name, s] = work.tile([P, BLOCK], F32, name=name)
                 jobs.append((s, gate, OP_SUM, func, live[name, s][:]))
             return jobs
@@ -356,7 +385,8 @@ def tile_treelstm_pa_t_kernel(
             for n, piece in enumerate(pieces):
                 nc.scalar.copy(out=c_out[:, n * width : (n + 1) * width, :], in_=piece)
             store(s, c_out, c_rows)
-            live["back_o", s] = transpose_back(s, "gate_o")
+            if ("gate_o", s) in live:
+                live["back_o", s] = transpose_back(s, "gate_o")
             unfinished.append(s)
 
         for t in range(STEPS):
@@ -380,6 +410,9 @@ def tile_treelstm_pa_t_kernel(
             jobs = []
             for s in gated:
                 jobs.extend(gate_jobs(s))
+            o_row = t - (FTILES * (BLOCKS - 1) - 2)
+            if 0 <= o_row < TILES:
+                jobs.append((o_row,))
             if t > 0:
                 new_forget(t)
                 jobs.extend([forget_job(t, k) for k in range(KIDS)])
@@ -390,12 +423,18 @@ def tile_treelstm_pa_t_kernel(
                     multiply_iu(s, nc.vector, work)
             if t == 1:
                 spread_bias(1, 1, 3)
+                o_bias_bank = banks.tile([P, FEAT], F32, name="o_bias_bank", tag="bank")
+                nc.tensor.matmul(out=o_bias_bank[:], lhsT=ones[:], rhs=o_bias_rows[:], start=True, stop=True)
+                nc.vector.tensor_copy(out=o_bias[:], in_=o_bias_bank[:])
             coming = units_of_round(t + 1)
             to_sort = [c for c in coming if c % 2 == 0 and c + 1 in coming]
             for count in [c for c in coming if c not in to_sort and c - 1 not in to_sort]:
                 sort_units(count, 1)
             for s in finished:
                 nc.vector.tensor_tensor(out=live["iu", s][:], in0=live["iu", s][:], in1=live["early_pair", s][:], op=ALU.add)
+            if 0 <= o_row < TILES:
+                nc.vector.tensor_tensor(out=o_last[:, o_row, :], in0=live["z_o", o_row][:], in1=o_bias[:], op=ALU.add)
+                nc.scalar.activation(out=o_last[:, o_row, :], in_=o_last[:, o_row, :], func=ACT.Sigmoid)
             late_data = t + 1 < FTILES
             if not late_data:
                 for count in to_sort:

from contextlib import ExitStack

import concourse.mybir as mybir
from concourse.masks import make_identity

F32 = mybir.dt.float32
BF16 = mybir.dt.bfloat16
I32 = mybir.dt.int32
U32 = mybir.dt.uint32
U8 = mybir.dt.uint8
FP8X4 = mybir.dt.float8_e4m3fn_x4
ACT = mybir.ActivationFunctionType
ALU = mybir.AluOpType

P = 128
NODES, FEAT, KIDS = 2048, 512, 4
PACK = 4
ROWS = NODES // P
BLOCK = 512
TILES = BLOCK // P
BLOCKS = NODES // BLOCK
FTILES = FEAT // P
STEPS = BLOCKS * FTILES
WORDS = FEAT // 2

GATE_I, GATE_F, GATE_U, GATE_O = 0, 1, 2, 3
GATES = 4
X_SIDE, H_SIDE = 0, 1

OP_X, OP_KID0, OP_SUM = 0, 1, 1 + KIDS
OPERANDS = 2 + KIDS
HALF = BLOCK // 2
UNITS = 2 * OPERANDS
UNITS_PER_STEP = UNITS // FTILES
AHEAD = UNITS

FLOPS = 2 * FEAT * FEAT * (7 * NODES + KIDS * NODES)


def tile_treelstm_pa_t_kernel(
    tc, inputs, child_c, child_h, child_h_sum,
    W_ix_words, W_ix_scales, b_ix, W_fx_words, W_fx_scales, b_fx,
    W_ux_words, W_ux_scales, b_ux, W_ox_words, W_ox_scales, b_ox,
    W_ih_words, W_ih_scales, b_ih, W_fh_words, W_fh_scales, b_fh,
    W_uh_words, W_uh_scales, b_uh, W_oh_words, W_oh_scales, b_oh,
    out_0, out_1,
):
    nc = tc.nc
    given_words = [W_ix_words, W_fx_words, W_ux_words, W_ox_words, W_ih_words, W_fh_words, W_uh_words, W_oh_words]
    given_scales = [W_ix_scales, W_fx_scales, W_ux_scales, W_ox_scales, W_ih_scales, W_fh_scales, W_uh_scales, W_oh_scales]
    given_bias = [b_ix, b_fx, b_ux, b_ox, b_ih, b_fh, b_uh, b_oh]

    kid_h_rows = child_h.rearrange("k (p r) d -> k p r d", r=ROWS)
    kid_c_rows = child_c.rearrange("k (p r) d -> k p r d", r=ROWS)
    operand_rows = (
        [inputs.rearrange("(p r) d -> p r d", r=ROWS)]
        + [kid_h_rows[k] for k in range(KIDS)]
        + [child_h_sum.rearrange("(p r) d -> p r d", r=ROWS)]
    )
    c_rows = out_0.rearrange("(p r) d -> p r d", r=ROWS)
    h_rows = out_1.rearrange("(p r) d -> p r d", r=ROWS)

    with ExitStack() as ctx:
        const = ctx.enter_context(tc.tile_pool(name="const", bufs=1))
        loads = ctx.enter_context(tc.tile_pool(name="loads", bufs=2))
        regroup = ctx.enter_context(tc.tile_pool(name="regroup", bufs=4))
        sorting = ctx.enter_context(tc.tile_pool(name="sorting", bufs=2))
        quant = ctx.enter_context(tc.tile_pool(name="quant", bufs=2))
        work = ctx.enter_context(tc.tile_pool(name="work", bufs=2))
        turn = ctx.enter_context(tc.tile_pool(name="turn", bufs=1))
        stores = ctx.enter_context(tc.tile_pool(name="stores", bufs=4))
        banks = ctx.enter_context(tc.psum_pool(name="banks", bufs=8))
        mx_banks = banks
        ct_banks = banks
        tp_banks = banks
        ctx.enter_context(tc.manual_schedule())

        w_words = const.tile([P, 2 * GATES, FEAT], U32, name="w_words", align_bytes=64)
        w_scales = const.tile([P, 2 * GATES, FEAT], U8, name="w_scales", align_bytes=64)
        ident_f32 = const.tile([P, P], F32, name="ident_f32")
        ident_bf16 = const.tile([P, P], BF16, name="ident_bf16")
        bias_rows = const.tile([P, 2, P], BF16, name="bias_rows")
        bias_cols = const.tile([P, 2, GATES * FTILES], F32, name="bias_cols")
        bias = const.tile([P, GATES, FTILES], F32, name="bias")
        warm = const.tile([P, 2], F32, name="warm")
        ones = const.tile([P, P], BF16, name="ones")
        o_bias_rows = const.tile([P, FEAT], BF16, name="o_bias_rows")
        o_bias = const.tile([P, FEAT], F32, name="o_bias")
        o_last = const.tile([P, TILES, FEAT], F32, name="o_last")

        nc.vector.memset(warm[:], 0.0)
        nc.vector.memset(bias_rows[:], 0.0)
        nc.vector.memset(w_scales[:].bitcast(I32), 0)
        nc.vector.memset(ones[:], 1.0)
        nc.vector.memset(o_bias_rows[:], 0.0)
        for row, vector in ((0, b_fx), (FTILES, b_fh)):
            nc.scalar.dma_start(out=bias_rows[row : row + FTILES, 0, :], in_=vector.rearrange("(m f) -> m f", f=P))
        nc.scalar.activation(out=warm[:, 1:2], in_=warm[:, 0:1], func=ACT.Sigmoid)
        make_identity(nc, ident_f32[:])
        nc.scalar.copy(out=ident_bf16[:], in_=ident_f32[:])

        operands = {}
        cells = {}

        def prep_order(b):
            kids = [OP_KID0 + k for k in range(KIDS)]
            return [OP_X] + kids + [OP_SUM] if b == 0 else [OP_X, OP_SUM] + kids

        def new_loads(b):
            operands[b] = loads.tile([P, OPERANDS, TILES, FEAT], BF16, name="operands")

        def load_operand(b, a):
            nc.sync.dma_start(out=operands[b][:, a, :, :], in_=operand_rows[a][:, b * TILES : (b + 1) * TILES, :])

        def new_cells(b):
            cells[b] = loads.tile([P, KIDS, TILES, FEAT], BF16, name="cells")

        def load_cell(b, k):
            nc.sync.dma_start(out=cells[b][:, k, :, :], in_=kid_c_rows[k][:, b * TILES : (b + 1) * TILES, :])

        def load_weight(slot):
            nc.sync.dma_start(
                out=w_words[:, slot, :].bitcast(I32),
                in_=given_words[slot][0].rearrange("p n t -> p (n t)").bitcast(I32),
            )

        def load_scales(slot, quadrant):
            nc.sync.dma_start(
                out=w_scales[32 * quadrant : 32 * quadrant + 4, slot, :].bitcast(I32),
                in_=given_scales[slot][0].bitcast(I32)[4 * quadrant : 4 * quadrant + 4, :],
            )

        def load_bias(queue, group, row, slot):
            queue.dma_start(out=bias_rows[row : row + FTILES, group, :], in_=given_bias[slot].rearrange("(m f) -> m f", f=P))

        new_loads(0)
        new_cells(0)
        new_loads(1)
        gate_order = (GATE_F, GATE_I, GATE_U, GATE_O)
        slots = [side * GATES + gate for gate in gate_order for side in (H_SIDE, X_SIDE)]
        scale_jobs = [(slot, quadrant) for slot in slots for quadrant in range(4)]
        large = (
            [(load_operand, 0, OP_X), (load_operand, 0, OP_KID0), (load_operand, 0, OP_KID0 + 1), (load_weight, slots[0]), (load_weight, slots[1])]
            + [(load_operand, 0, OP_KID0 + k) for k in range(2, KIDS)]
            + [(load_operand, 0, OP_SUM)]
            + [(load_cell, 0, k) for k in range(KIDS)]
            + [(load_weight, slot) for slot in slots[2:]]
            + [(load_operand, 1, a) for a in prep_order(1)]
        )
        for n, job in enumerate(large):
            job[0](*job[1:])
            for slot, quadrant in scale_jobs[2 * n : 2 * n + 2]:
                load_scales(slot, quadrant)
        for n, gate in enumerate(gate_order[1:]):
            load_bias(nc.gpsimd, 1, n * FTILES, X_SIDE * GATES + gate)
            load_bias(nc.gpsimd, 1, (3 + n) * FTILES, H_SIDE * GATES + gate)
        for row, vector in enumerate((b_ox, b_oh)):
            nc.gpsimd.dma_start(out=o_bias_rows[row : row + 1, :], in_=vector.rearrange("(o f) -> o f", o=1))

        q_words = {}
        q_scales = {}

        def new_quantised(b):
            q_words[b] = quant.tile([P, OPERANDS, BLOCK], U32, name="q_words", align_bytes=64)
            q_scales[b] = quant.tile([P, OPERANDS, BLOCK], U8, name="q_scales", align_bytes=64)

        sorted_words = {}

        def sort_units(count, units):
            b, unit = divmod(count, UNITS)
            first_row = 2 * (unit % 2)
            if units == 2:
                words = sorting.tile([P, 2 * units, 2, P], F32, name="words", bufs=4)
            else:
                words = sorting.tile([P, 2 * units, 2, P], F32, name="half_words")
            rows = operands[b][:, prep_order(b)[unit // 2], first_row : first_row + 2 * units, :]
            nc.vector.tensor_copy(out=words[:], in_=rows.bitcast(F32).rearrange("n j (p u) -> n j u p", u=2))
            for n in range(units):
                sorted_words[count + n] = words[:, 2 * n : 2 * n + 2, :, :]

        def transpose_unit(count):
            b, unit = divmod(count, UNITS)
            a, half = prep_order(b)[unit // 2], unit % 2
            bank = tp_banks.tile([P, 2, 2, P], F32, name="xt", tag="bank")
            for j in range(2):
                row_words = operands[b][:, a, 2 * half + j, :].bitcast(F32)
                for u in range(2):
                    words = sorted_words[count][:, j, u, :] if count in sorted_words else row_words[:, u:WORDS:2]
                    nc.tensor.transpose(out=bank[:, j, u, :], in_=words, identity=ident_f32[:])
            return bank

        def regroup_unit(copy, bank):
            grouped = regroup.tile([P, HALF, PACK], BF16, name="grouped", align_bytes=64)
            as_words = grouped[:].rearrange("p c t -> p (c t)").bitcast(F32)
            copy(out=as_words.rearrange("p (j r u) -> p j r u", j=2, u=2), in_=bank[:].rearrange("p j u r -> p j r u"))
            return grouped

        def quantise_unit(count, grouped):
            b, unit = divmod(count, UNITS)
            a, half = prep_order(b)[unit // 2], unit % 2
            if unit == 0:
                new_quantised(b)
            cols = slice(half * HALF, (half + 1) * HALF)
            nc.vector.quantize_mx(
                out=q_words[b][:, a, cols].bitcast(FP8X4),
                scales=q_scales[b][:, a, cols],
                in_=grouped[:].rearrange("p c t -> p (c t)"),
            )

        live = {}

        def mx_group(t, gate, h_operand):
            b, m = divmod(t, FTILES)
            feats = slice(m * P, (m + 1) * P)
            z = mx_banks.tile([P, BLOCK], F32, name="z", tag="bank")
            for side, a in ((H_SIDE, h_operand), (X_SIDE, OP_X)):
                slot = side * GATES + gate
                nc.tensor.matmul_mx(
                    out=z[:],
                    lhsT=w_words[:, slot, feats].bitcast(FP8X4),
                    lhsT_scale=w_scales[:, slot, feats],
                    rhs=q_words[b][:, a, :].bitcast(FP8X4),
                    rhs_scale=q_scales[b][:, a, :],
                    start=(side == H_SIDE),
                    stop=(side == X_SIDE),
                )
            return z

        def o_group(j):
            nodes = slice(j * P, (j + 1) * P)
            z = banks.tile([P, FEAT], F32, name="z_o", tag="bank")
            for side, a in ((H_SIDE, OP_SUM), (X_SIDE, OP_X)):
                slot = side * GATES + GATE_O
                nc.tensor.matmul_mx(
                    out=z[:],
                    lhsT=q_words[BLOCKS - 1][:, a, nodes].bitcast(FP8X4),
                    lhsT_scale=q_scales[BLOCKS - 1][:, a, nodes],
                    rhs=w_words[:, slot, :].bitcast(FP8X4),
                    rhs_scale=w_scales[:, slot, :],
                    start=(side == H_SIDE),
                    stop=(side == X_SIDE),
                )
            live["z_o", j] = z
            return z

        def squash(t, gate, func, z, out):
            m = t % FTILES
            nc.scalar.activation(out=out, in_=z[:], func=func, bias=bias[:, gate_order.index(gate), m : m + 1])

        def transpose_cells(t, pair):
            b, m = divmod(t, FTILES)
            bank = ct_banks.tile([P, 2, TILES, P], BF16, name="ct", tag="bank")
            for k in range(2):
                for j in range(TILES):
                    nc.tensor.matmul(
                        out=bank[:, k, j, :],
                        lhsT=cells[b][:, 2 * pair + k, j, m * P : (m + 1) * P],
                        rhs=ident_bf16[:],
                        start=True,
                        stop=True,
                    )
            live["ct", t, pair] = bank

        def products(t, pair):
            kids = slice(2 * pair, 2 * pair + 2)
            nc.vector.tensor_tensor(
                out=live["forget", t][:, kids, :],
                in0=live["forget", t][:, kids, :],
                in1=live["ct", t, pair][:].rearrange("p k j r -> p k (j r)"),
                op=ALU.mult,
            )

        def transpose_back(t, name):
            bank = tp_banks.tile([P, TILES, P], F32, name="back", tag="bank")
            for j in range(TILES):
                nc.tensor.transpose(out=bank[:, j, :], in_=live[name, t][:, j * P : (j + 1) * P], identity=ident_f32[:])
            return bank

        def store(t, node_major, dram):
            b, m = divmod(t, FTILES)
            nc.sync.dma_start(out=dram[:, b * TILES : (b + 1) * TILES, m * P : (m + 1) * P], in_=node_major[:])

        def spread_bias(group, first, gates):
            width = gates * FTILES
            bias_bank = tp_banks.tile([P, P], BF16, name="bias_bank", tag="bank")
            nc.tensor.transpose(out=bias_bank[:], in_=bias_rows[:, group, :], identity=ident_bf16[:])
            nc.vector.tensor_copy(out=bias_cols[:, :, 0:width], in_=bias_bank[:, 0 : 2 * width].rearrange("p (s c) -> p s c", s=2))
            nc.vector.tensor_tensor(
                out=bias[:, first : first + gates, :].rearrange("p g m -> p (g m)"),
                in0=bias_cols[:, X_SIDE, 0:width],
                in1=bias_cols[:, H_SIDE, 0:width],
                op=ALU.add,
            )

        lagging = []

        def flush():
            for count, grouped in lagging:
                quantise_unit(count, grouped)
            lagging.clear()

        def prepare(count, copy):
            grouped = regroup_unit(copy, transpose_unit(count))
            flush()
            lagging.append((count, grouped))

        def new_forget(t):
            live["forget", t] = work.tile([P, KIDS, BLOCK], F32, name="forget")

        def forget_job(t, k):
            return (t, GATE_F, OP_KID0 + k, ACT.Sigmoid, live["forget", t][:, k, :])

        def run_jobs(jobs):
            sums = []
            for n in range(len(jobs) + 3):
                if n >= 3 and len(jobs[n - 3]) > 1:
                    done = jobs[n - 3]
                    squash(done[0], done[1], done[3], sums[n - 3], done[4])
                if n < len(jobs):
                    sums.append(mx_group(jobs[n][0], jobs[n][1], jobs[n][2]) if len(jobs[n]) > 1 else o_group(jobs[n][0]))

        new_forget(0)
        for count in range(AHEAD):
            prepare(count, nc.scalar.copy if count % 2 == 0 else nc.vector.tensor_copy)
            if count == 1:
                spread_bias(0, 0, 1)
            if count % 2 == 1 and count >= 5:
                run_jobs([forget_job(0, (count - 5) // 2)])
        flush()

        def units_of_round(t):
            if t < 2:
                return []
            if t < FTILES:
                return list(range(UNITS + UNITS // 2 * (t - 2), UNITS + UNITS // 2 * (t - 1)))
            first = 2 * UNITS + UNITS_PER_STEP * (t - FTILES)
            return [c for c in range(first, first + UNITS_PER_STEP) if c < BLOCKS * UNITS]

        def gate_steps(t):
            if t < 2 or t == STEPS - 1:
                return []
            if t < FTILES:
                return [2 * (t - 2), 2 * (t - 2) + 1]
            return [t]

        def finish_steps(t):
            if t < 2:
                return []
            return [0, 1] if t == 2 else [t - 1]

        unfinished = []

        def finish_hidden():
            for s in unfinished:
                h_out = stores.tile([P, TILES, P], F32, name="h_out")
                o_gate = live["back_o", s][:] if ("back_o", s) in live else o_last[:, :, (s % FTILES) * P : (s % FTILES + 1) * P]
                nc.vector.tensor_tensor(out=h_out[:], in0=live["tanh_c", s][:], in1=o_gate, op=ALU.mult)
                store(s, h_out, h_rows)
            unfinished.clear()

        def gate_jobs(s):
            jobs = []
            gates = [("gate_i", GATE_I, ACT.Sigmoid), ("gate_u", GATE_U, ACT.Tanh)]
            if s // FTILES < BLOCKS - 1:
                gates.append(("gate_o", GATE_O, ACT.Sigmoid))
            for name, gate, func in gates:
                live[name, s] = work.tile([P, BLOCK], F32, name=name)
                jobs.append((s, gate, OP_SUM, func, live[name, s][:]))
            return jobs

        def multiply_iu(s, engine, pool):
            live["iu", s] = pool.tile([P, BLOCK], F32, name="iu")
            engine.tensor_tensor(out=live["iu", s][:], in0=live["gate_i", s][:], in1=live["gate_u", s][:], op=ALU.mult)

        def add_pair(s, name, engine, first):
            live[name, s] = work.tile([P, BLOCK], F32, name=name)
            engine.tensor_tensor(out=live[name, s][:], in0=live["forget", s][:, first, :], in1=live["forget", s][:, first + 1, :], op=ALU.add)

        def leave(s, pieces):
            live["tanh_c", s] = work.tile([P, TILES, P], F32, name="tanh_c")
            c_out = stores.tile([P, TILES, P], F32, name="c_out")
            width = TILES // len(pieces)
            for n, piece in enumerate(pieces):
                nc.scalar.activation(out=live["tanh_c", s][:, n * width : (n + 1) * width, :], in_=piece, func=ACT.Tanh)
            for n, piece in enumerate(pieces):
                nc.scalar.copy(out=c_out[:, n * width : (n + 1) * width, :], in_=piece)
            store(s, c_out, c_rows)
            if ("gate_o", s) in live:
                live["back_o", s] = transpose_back(s, "gate_o")
            unfinished.append(s)

        for t in range(STEPS):
            b, m = divmod(t, FTILES)
            counts = units_of_round(t)
            gated = gate_steps(t)
            finished = finish_steps(t)
            if m == 1 and b + 1 < BLOCKS:
                new_cells(b + 1)
                for k in range(KIDS):
                    load_cell(b + 1, k)
            if m == 2 and b + 2 < BLOCKS:
                new_loads(b + 2)
                for a in prep_order(b + 2):
                    load_operand(b + 2, a)

            if t > 0:
                add_pair(t - 1, "late_pair", nc.vector, 2)
            flush()

            jobs = []
            for s in gated:
                jobs.extend(gate_jobs(s))
            o_row = t - (FTILES * (BLOCKS - 1) - 2)
            if 0 <= o_row < TILES:
                jobs.append((o_row,))
            if t > 0:
                new_forget(t)
                jobs.extend([forget_job(t, k) for k in range(KIDS)])
            run_jobs(jobs)

            for s in finished:
                if ("iu", s) not in live:
                    multiply_iu(s, nc.vector, work)
            if t == 1:
                spread_bias(1, 1, 3)
                o_bias_bank = banks.tile([P, FEAT], F32, name="o_bias_bank", tag="bank")
                nc.tensor.matmul(out=o_bias_bank[:], lhsT=ones[:], rhs=o_bias_rows[:], start=True, stop=True)
                nc.vector.tensor_copy(out=o_bias[:], in_=o_bias_bank[:])
            coming = units_of_round(t + 1)
            to_sort = [c for c in coming if c % 2 == 0 and c + 1 in coming]
            for count in [c for c in coming if c not in to_sort and c - 1 not in to_sort]:
                sort_units(count, 1)
            for s in finished:
                nc.vector.tensor_tensor(out=live["iu", s][:], in0=live["iu", s][:], in1=live["early_pair", s][:], op=ALU.add)
            if 0 <= o_row < TILES:
                nc.vector.tensor_tensor(out=o_last[:, o_row, :], in0=live["z_o", o_row][:], in1=o_bias[:], op=ALU.add)
                nc.scalar.activation(out=o_last[:, o_row, :], in_=o_last[:, o_row, :], func=ACT.Sigmoid)
            late_data = t + 1 < FTILES
            if not late_data:
                for count in to_sort:
                    sort_units(count, 2)
            if late_data or not to_sort:
                finish_hidden()
            for s in finished:
                live["cell", s] = work.tile([P, BLOCK], F32, name="cell")
                nc.vector.tensor_tensor(out=live["cell", s][:], in0=live["late_pair", s][:], in1=live["iu", s][:], op=ALU.add)
            finish_hidden()
            for s in gated:
                if s not in finished:
                    multiply_iu(s, nc.gpsimd, turn)

            split = (len(counts) + 1) // 2
            one_run = len(counts) == UNITS_PER_STEP
            transpose_cells(t, 0)
            products(t, 0)
            if t < STEPS - 1:
                add_pair(t, "early_pair", nc.gpsimd, 0)
            if one_run:
                transpose_cells(t, 1)
                products(t, 1)
            for count in counts[:split]:
                prepare(count, nc.scalar.copy)
            if not one_run:
                transpose_cells(t, 1)
                products(t, 1)
            if t == STEPS - 1:
                run_jobs(gate_jobs(t))
            for s in finished:
                finish_hidden()
                leave(s, [transpose_back(s, "cell")[:]])
            for count in counts[split:]:
                prepare(count, nc.scalar.copy)
            if late_data:
                for count in to_sort:
                    sort_units(count, 2)

        last = STEPS - 1
        parts = [live["forget", last][:, k, :] for k in range(KIDS)]
        multiply_iu(last, nc.vector, work)
        parts.append(live["iu", last][:])
        pieces = []
        for j in range(TILES):
            piece = banks.tile([P, 1, P], F32, name="piece", tag="bank")
            pieces.append(piece)
        for n, part in enumerate(parts):
            for j in range(TILES):
                nc.tensor.matmul(
                    out=pieces[j][:, 0, :], lhsT=part[:, j * P : (j + 1) * P], rhs=ident_f32[:], is_transpose=True, start=(n == 0), stop=(n == len(parts) - 1)
                )
        finish_hidden()
        leave(last, [piece[:] for piece in pieces])
        finish_hidden()
